import numpy as np
import ml_dtypes


def mxq(x, axis, fmt="e4m3"):
    dtype, down = {"e4m3": (ml_dtypes.float8_e4m3fn, 7), "e5m2": (ml_dtypes.float8_e5m2, 14)}[fmt]
    v = np.moveaxis(np.asarray(x, np.float32).astype(ml_dtypes.bfloat16).astype(np.float64), axis, -1)
    blocks = v.reshape(v.shape[:-1] + (-1, 32))
    amax = np.abs(blocks).max(-1, keepdims=True)
    byte = np.maximum(np.where(amax > 0, np.frexp(amax)[1] - 1 + 127, 0) - down, 1)
    scale = np.exp2(byte - 127.0)
    codes = (blocks / scale).astype(np.float32).astype(dtype).astype(np.float64)
    return np.moveaxis((codes * scale).reshape(v.shape), -1, axis)


WIDE = False


def mx_kscale(k):
    if not WIDE:
        return np.ones(k)
    levels = np.array([10, -10, 5, -5, 0])
    a = np.random.permutation(np.resize(levels, k // 512 * 4)).reshape(k // 512, 4)
    idx = np.arange(k)
    return np.exp2(a[idx // 512, idx % 128 // 32])


BF16 = ml_dtypes.bfloat16


def bf(x):
    return np.asarray(x, np.float32).astype(BF16)


def f64(x):
    return np.asarray(x).astype(np.float64)


B, S, D, H = 8, 512, 512, 2
HD = D // H
NEG = -3.4028234663852886e38


def alibi_slopes(num_heads):
    ratio = 2.0 ** (-8.0 / num_heads)
    return ratio ** f64(np.arange(1, num_heads + 1))


def setup_inputs():
    s = mx_kscale(D)
    return {"x": bf(np.random.standard_normal((B, S, D)) * s),
            "Wv": bf(np.random.standard_normal((D, D)) / np.sqrt(D) / s[:, None]),
            "bv": bf(np.random.standard_normal(D) * 0.1),
            "q": bf(np.random.standard_normal((B, H, S, HD))),
            "k": bf(np.random.standard_normal((B, H, S, HD)))}


def reference(x, Wv, bv, q, k):
    v = (mxq(f64(x), 2, "e4m3") @ mxq(f64(Wv), 0, "e4m3")) + f64(bv)
    v = v.reshape(B, S, H, HD).transpose(0, 2, 1, 3)
    scores = f64(q) @ f64(k).transpose(0, 1, 3, 2) / np.sqrt(HD)
    distances = f64(np.arange(1 - S, 1))
    scores = scores + alibi_slopes(H)[None, :, None, None] * distances[None, None, None, :]
    causal = np.tril(np.ones((S, S), dtype=bool))[None, None]
    scores = np.where(causal, scores, NEG)
    e = np.exp(scores - scores.max(-1, keepdims=True))
    ctx = (mxq(e, 3, "e4m3") @ mxq(v, 2, "e4m3")) / e.sum(-1, keepdims=True)
    return ctx.transpose(0, 2, 1, 3).reshape(B, S, D)

@@ -1,0 +1,295 @@
+import math
+from contextlib import ExitStack
+
+import concourse.mybir as mybir
+from concourse.masks import make_identity
+
+F32 = mybir.dt.float32
+BF16 = mybir.dt.bfloat16
+I32 = mybir.dt.int32
+U32 = mybir.dt.uint32
+U8 = mybir.dt.uint8
+FP8X4 = mybir.dt.float8_e4m3fn_x4
+ALU = mybir.AluOpType
+ACT = mybir.ActivationFunctionType
+
+B, S, D, H = 8, 512, 512, 2
+HD = D // H
+P = 128
+PACK = 4
+Q_TILES = S // P
+HEADS = B * H
+SCORE_SCALE = 1.0 / math.sqrt(HD)
+MASKED = -3.0e38
+E_COPIES = 3
+
+FLOPS = 2 * B * S * D * D + 2 * (2 * B * H * S * S * HD)
+
+
+def tile_selfattention_pa_t_kernel(tc, x, Wv, bv, q, k, out):
+    nc = tc.nc
+    with ExitStack() as ctx:
+        const = ctx.enter_context(tc.tile_pool(name="const", bufs=1))
+        loads = ctx.enter_context(tc.tile_pool(name="loads", bufs=B))
+        work = ctx.enter_context(tc.tile_pool(name="work", bufs=2))
+        small = ctx.enter_context(tc.tile_pool(name="small", bufs=6))
+        psum = ctx.enter_context(tc.psum_pool(name="psum", bufs=1))
+
+        wv_raw = const.tile([P, PACK, D], BF16)
+        nc.scalar.dma_start(
+            out=wv_raw[:].rearrange("w (u e) n -> w u e n", u=2),
+            in_=Wv.rearrange("(u w e) n -> w u e n", u=2, e=2),
+        )
+        bv_all = const.tile([P, D], BF16)
+        nc.scalar.dma_start(out=bv_all[:], in_=bv.partition_broadcast(P))
+        x_rows, q_rows, k_rows = [], [], []
+        for b in range(B):
+            k_sb = loads.tile([P, H, 2, 2, HD], BF16)
+            nc.sync.dma_start(
+                out=k_sb[:], in_=k[b].rearrange("h (half r u) d -> r h half u d", half=2, u=2)
+            )
+            q_sb = loads.tile([P, H, Q_TILES, HD], BF16)
+            nc.sync.dma_start(out=q_sb[:], in_=q[b].rearrange("h (it p) d -> p h it d", p=P))
+            x_sb = loads.tile([P, PACK, D], BF16)
+            nc.sync.dma_start(out=x_sb[:], in_=x[b].rearrange("(p t) f -> p t f", t=PACK))
+            k_rows.append(k_sb)
+            q_rows.append(q_sb)
+            x_rows.append(x_sb)
+
+        ident_f32 = const.tile([P, P], F32)
+        make_identity(nc, ident_f32[:])
+        ident_bf16 = const.tile([P, P], BF16)
+        make_identity(nc, ident_bf16[:])
+
+        key_pos = const.tile([P, S], I32)
+        nc.gpsimd.iota(key_pos[:], pattern=[[1, 2], [4, P], [2, 2]], base=-(S // 2), channel_multiplier=0)
+        bias_f32 = const.tile([P, S], F32)
+        nc.vector.tensor_copy(out=bias_f32[:], in_=key_pos[:])
+        nc.gpsimd.affine_select(
+            out=bias_f32[:],
+            in_=bias_f32[:],
+            pattern=[[-1, 2], [-4, P], [-2, 2]],
+            compare_op=ALU.is_ge,
+            fill=MASKED,
+            base=S - P,
+            channel_multiplier=1,
+        )
+        bias_of_head = []
+        for h in range(H):
+            slope = 2.0 ** (-8.0 / H * (h + 1))
+            bias_bf16 = const.tile([P, S], BF16, name="bias_bf16_%d" % h)
+            nc.vector.tensor_scalar_mul(out=bias_bf16[:], in0=bias_f32[:], scalar1=slope / SCORE_SCALE)
+            bias_of_head.append(bias_bf16)
+
+        e_tiles = []
+        for i in range(E_COPIES):
+            e_sb = const.tile([P, Q_TILES, 2, S // 2], BF16, name="e_sb_%d" % i)
+            nc.vector.memset(e_sb[:], 0.0)
+            e_tiles.append(e_sb)
+
+        wv_grouped = const.tile([P, D, PACK], BF16, align_bytes=64)
+        nc.vector.tensor_copy(out=wv_grouped[:], in_=wv_raw[:].rearrange("w t n -> w n t"))
+        wv_codes = const.tile([P, D], U32, align_bytes=64)
+        wv_scales = const.tile([P, D], U8, align_bytes=64)
+        nc.vector.quantize_mx(
+            out=wv_codes[:].bitcast(FP8X4),
+            scales=wv_scales[:],
+            in_=wv_grouped[:].rearrange("w n t -> w (n t)"),
+        )
+
+        x_mx, v_mx, qk_t, e_of, e_mx, sums = {}, {}, {}, {}, {}, {}
+
+        def prepare_x(b):
+            x_grouped = work.tile([P, PACK * S], BF16, align_bytes=64)
+            x_words = x_grouped[:].bitcast(F32).rearrange("w (t c u) -> w t c u", t=PACK, u=2)
+            for pair in range(2):
+                xt_ps = psum.tile([P, 2, 2, P], F32, tag="prep", bufs=2)
+                for tl in range(2):
+                    t = 2 * pair + tl
+                    row = 2 * (t % 2) + t // 2
+                    for u in range(2):
+                        nc.tensor.transpose(
+                            out=xt_ps[:, tl, u, :],
+                            in_=x_rows[b][:, row, :].bitcast(F32)[:, P * u : P * (u + 1)],
+                            identity=ident_f32[:],
+                        )
+                nc.vector.tensor_copy(
+                    out=x_words[:, 2 * pair : 2 * pair + 2],
+                    in_=xt_ps[:].rearrange("w t u c -> w t c u"),
+                )
+            x_codes = work.tile([P, S], U32, align_bytes=64)
+            x_scales = work.tile([P, S], U8, align_bytes=64)
+            nc.vector.quantize_mx(out=x_codes[:].bitcast(FP8X4), scales=x_scales[:], in_=x_grouped[:])
+            x_mx[b] = (x_codes, x_scales)
+
+        def project_v(b):
+            x_codes, x_scales = x_mx[b]
+            v_grouped = work.tile([P, D, PACK], BF16, align_bytes=64)
+            for c in range(D // P):
+                cols = slice(P * c, P * (c + 1))
+                v_ps = psum.tile([P, PACK, P], F32, tag="prep", bufs=2)
+                for t in range(PACK):
+                    keys = slice(P * t, P * (t + 1))
+                    nc.tensor.matmul_mx(
+                        out=v_ps[:, t, :],
+                        lhsT=x_codes[:, keys].bitcast(FP8X4),
+                        lhsT_scale=x_scales[:, keys],
+                        rhs=wv_codes[:, cols].bitcast(FP8X4),
+                        rhs_scale=wv_scales[:, cols],
+                        start=True,
+                        stop=True,
+                    )
+                nc.vector.tensor_tensor(
+                    out=v_grouped[:, cols, :],
+                    in0=v_ps[:].rearrange("p t n -> p n t"),
+                    in1=bv_all[:, cols].unsqueeze(2).to_broadcast([P, P, PACK]),
+                    op=ALU.add,
+                )
+            v_codes = work.tile([P, D], U32, align_bytes=64, bufs=3)
+            v_scales = work.tile([P, D], U8, align_bytes=64, bufs=3)
+            nc.vector.quantize_mx(
+                out=v_codes[:].bitcast(FP8X4),
+                scales=v_scales[:],
+                in_=v_grouped[:].rearrange("p n t -> p (n t)"),
+            )
+            v_mx[b] = (v_codes, v_scales)
+
+        def prepare_qk(n):
+            b, h = n // H, n % H
+            qt_ps = psum.tile([P, Q_TILES, P], F32, tag="prep", bufs=2)
+            for it in range(Q_TILES):
+                nc.tensor.transpose(
+                    out=qt_ps[:, it, :], in_=q_rows[b][:, h, it, :].bitcast(F32), identity=ident_f32[:]
+                )
+            q_t = work.tile([P, 2 * S], BF16, bufs=3)
+            nc.scalar.copy(out=q_t[:], in_=qt_ps[:].rearrange("w a i -> w (a i)").bitcast(BF16))
+            kt_ps = psum.tile([P, 2, 2, P], F32, tag="prep", bufs=2)
+            for u in range(2):
+                for half in range(2):
+                    nc.tensor.transpose(
+                        out=kt_ps[:, u, half, :],
+                        in_=k_rows[b][:, h, half, u, :].bitcast(F32),
+                        identity=ident_f32[:],
+                    )
+            k_t = work.tile([P, 2 * S], BF16, bufs=3)
+            nc.scalar.copy(out=k_t[:], in_=kt_ps[:].rearrange("w u a r -> w (u a r)").bitcast(BF16))
+            qk_t[n] = (q_t, k_t)
+
+        def attend(n):
+            h = n % H
+            q_t, k_t = qk_t[n]
+            q_view = q_t[:].rearrange("w (a i e) -> w a i e", a=Q_TILES, e=2)
+            k_view = k_t[:].rearrange("w (u c e) -> w u c e", u=2, e=2)
+            bias_view = bias_of_head[h][:].rearrange("i (u c) -> i u c", u=2)
+            e_sb = e_tiles[n % E_COPIES]
+            row_sum = small.tile([P, Q_TILES], F32)
+            for it in range(Q_TILES):
+                width = (P // 2) * (it + 1)
+                s_ps = psum.tile([P, S], F32, tag="scores", bufs=3)
+                s_view = s_ps[:, : 2 * width].rearrange("i (u c) -> i u c", u=2)
+                for e in range(2):
+                    nc.tensor.matmul(
+                        out=s_view,
+                        lhsT=q_view[:, it, :, e],
+                        rhs=k_view[:, :, :width, e],
+                        start=(e == 0),
+                        stop=False,
+                    )
+                nc.tensor.matmul(
+                    out=s_view,
+                    lhsT=ident_bf16[:],
+                    rhs=bias_view[:, :, S // 2 - width :],
+                    start=False,
+                    stop=True,
+                )
+                unread = small.tile([P, S], BF16)
+                neg_max = small.tile([P, 1], F32)
+                nc.vector.tensor_scalar(
+                    out=unread[:, : 2 * width],
+                    in0=s_ps[:, : 2 * width],
+                    scalar1=-SCORE_SCALE,
+                    scalar2=None,
+                    op0=ALU.mult,
+                    op1=ALU.min,
+                    accum_out=neg_max[:],
+                )
+                nc.scalar.activation(
+                    out=e_sb[:, it, :, :width],
+                    in_=s_view,
+                    func=ACT.Exp,
+                    bias=neg_max[:],
+                    scale=SCORE_SCALE,
+                    accum_out=row_sum[:, it : it + 1],
+                )
+            e_of[n] = e_sb
+            sums[n] = row_sum
+
+        def transpose_e(n):
+            e_sb = e_of[n]
+            e_grouped = work.tile([P, PACK * S], BF16, align_bytes=64)
+            e_words = e_grouped[:].bitcast(F32).rearrange("p (a i u) -> p a i u", a=Q_TILES, u=2)
+            for pair in range(Q_TILES // 2):
+                et_ps = psum.tile([P, 2, 2, P], F32, tag="tail", bufs=3)
+                for a in range(2):
+                    for u in range(2):
+                        nc.tensor.transpose(
+                            out=et_ps[:, a, u, :],
+                            in_=e_sb[:, 2 * pair + a, u, :].bitcast(F32),
+                            identity=ident_f32[:],
+                        )
+                nc.scalar.copy(
+                    out=e_words[:, 2 * pair : 2 * pair + 2],
+                    in_=et_ps[:].rearrange("p a u i -> p a i u"),
+                )
+            e_codes = work.tile([P, S], U32, align_bytes=64)
+            e_scales = work.tile([P, S], U8, align_bytes=64)
+            nc.vector.quantize_mx(out=e_codes[:].bitcast(FP8X4), scales=e_scales[:], in_=e_grouped[:])
+            e_mx[n] = (e_codes, e_scales)
+
+        def context(n):
+            b, h = n // H, n % H
+            e_codes, e_scales = e_mx[n]
+            v_codes, v_scales = v_mx[b]
+            dims = slice(HD * h, HD * (h + 1))
+            inv_sum = small.tile([P, Q_TILES], F32)
+            nc.vector.reciprocal(out=inv_sum[:], in_=sums[n][:])
+            ctx_sb = work.tile([P, Q_TILES, HD], F32, bufs=4)
+            for pair in range(Q_TILES // 2):
+                c_ps = psum.tile([P, 2, HD], F32, tag="tail", bufs=3)
+                for a in range(2):
+                    queries = slice(P * (2 * pair + a), P * (2 * pair + a + 1))
+                    nc.tensor.matmul_mx(
+                        out=c_ps[:, a, :],
+                        lhsT=e_codes[:, queries].bitcast(FP8X4),
+                        lhsT_scale=e_scales[:, queries],
+                        rhs=v_codes[:, dims].bitcast(FP8X4),
+                        rhs_scale=v_scales[:, dims],
+                        start=True,
+                        stop=True,
+                    )
+                for a in range(2):
+                    it = 2 * pair + a
+                    nc.scalar.activation(
+                        out=ctx_sb[:, it, :], in_=c_ps[:, a, :], func=ACT.Copy, scale=inv_sum[:, it : it + 1]
+                    )
+            nc.sync.dma_start(
+                out=out[b, :, dims].rearrange("(it p) d -> p it d", p=P), in_=ctx_sb[:]
+            )
+
+        prepare_qk(0)
+        prepare_x(0)
+        prepare_qk(1)
+        project_v(0)
+        for n in range(HEADS + 2):
+            if n < HEADS:
+                attend(n)
+            if 1 <= n <= HEADS:
+                transpose_e(n - 1)
+            if n + 2 < HEADS:
+                prepare_qk(n + 2)
+            if n % 2 == 0 and n // 2 + 1 < B:
+                prepare_x(n // 2 + 1)
+            if n >= 2:
+                context(n - 2)
+            if n % 2 == 1 and n // 2 + 1 < B:
+                project_v(n // 2 + 1)

@@ -22,6 +22,7 @@ HEADS = B * H
 SCORE_SCALE = 1.0 / math.sqrt(HD)
 MASKED = -3.0e38
 E_COPIES = 3
+PSUM_BANKS = 8
 
 FLOPS = 2 * B * S * D * D + 2 * (2 * B * H * S * S * HD)
 
@@ -30,10 +31,10 @@ def tile_selfattention_pa_t_kernel(tc, x, Wv, bv, q, k, out):
     nc = tc.nc
     with ExitStack() as ctx:
         const = ctx.enter_context(tc.tile_pool(name="const", bufs=1))
-        loads = ctx.enter_context(tc.tile_pool(name="loads", bufs=B))
+        loads = ctx.enter_context(tc.tile_pool(name="loads", bufs=HEADS))
         work = ctx.enter_context(tc.tile_pool(name="work", bufs=2))
         small = ctx.enter_context(tc.tile_pool(name="small", bufs=6))
-        psum = ctx.enter_context(tc.psum_pool(name="psum", bufs=1))
+        psum = ctx.enter_context(tc.psum_pool(name="psum", bufs=PSUM_BANKS))
 
         wv_raw = const.tile([P, PACK, D], BF16)
         nc.scalar.dma_start(
@@ -44,17 +45,18 @@ def tile_selfattention_pa_t_kernel(tc, x, Wv, bv, q, k, out):
         nc.scalar.dma_start(out=bv_all[:], in_=bv.partition_broadcast(P))
         x_rows, q_rows, k_rows = [], [], []
         for b in range(B):
-            k_sb = loads.tile([P, H, 2, 2, HD], BF16)
-            nc.sync.dma_start(
-                out=k_sb[:], in_=k[b].rearrange("h (half r u) d -> r h half u d", half=2, u=2)
-            )
-            q_sb = loads.tile([P, H, Q_TILES, HD], BF16)
-            nc.sync.dma_start(out=q_sb[:], in_=q[b].rearrange("h (it p) d -> p h it d", p=P))
-            x_sb = loads.tile([P, PACK, D], BF16)
+            x_sb = loads.tile([P, PACK, D], BF16, bufs=B)
             nc.sync.dma_start(out=x_sb[:], in_=x[b].rearrange("(p t) f -> p t f", t=PACK))
-            k_rows.append(k_sb)
-            q_rows.append(q_sb)
             x_rows.append(x_sb)
+            for h in range(H):
+                q_sb = loads.tile([P, Q_TILES, HD], BF16)
+                nc.sync.dma_start(out=q_sb[:], in_=q[b, h].rearrange("(it p) d -> p it d", p=P))
+                q_rows.append(q_sb)
+                k_sb = loads.tile([P, 2, 2, HD], BF16)
+                nc.sync.dma_start(
+                    out=k_sb[:], in_=k[b, h].rearrange("(half r u) d -> r half u d", half=2, u=2)
+                )
+                k_rows.append(k_sb)
 
         ident_f32 = const.tile([P, P], F32)
         make_identity(nc, ident_f32[:])
@@ -97,37 +99,57 @@ def tile_selfattention_pa_t_kernel(tc, x, Wv, bv, q, k, out):
             in_=wv_grouped[:].rearrange("w n t -> w (n t)"),
         )
 
-        x_mx, v_mx, qk_t, e_of, e_mx, sums = {}, {}, {}, {}, {}, {}
+        x_grouped_of, x_mx, v_grouped_of, v_mx = {}, {}, {}, {}
+        q_t_of, k_t_of, s_of, neg_max_of, sums = {}, {}, {}, {}, {}
+        e_grouped_of, e_mx, inv_of, ctx_of = {}, {}, {}, {}
 
-        def prepare_x(b):
-            x_grouped = work.tile([P, PACK * S], BF16, align_bytes=64)
-            x_words = x_grouped[:].bitcast(F32).rearrange("w (t c u) -> w t c u", t=PACK, u=2)
-            for pair in range(2):
-                xt_ps = psum.tile([P, 2, 2, P], F32, tag="prep", bufs=2)
-                for tl in range(2):
-                    t = 2 * pair + tl
-                    row = 2 * (t % 2) + t // 2
-                    for u in range(2):
-                        nc.tensor.transpose(
-                            out=xt_ps[:, tl, u, :],
-                            in_=x_rows[b][:, row, :].bitcast(F32)[:, P * u : P * (u + 1)],
-                            identity=ident_f32[:],
-                        )
-                nc.vector.tensor_copy(
-                    out=x_words[:, 2 * pair : 2 * pair + 2],
-                    in_=xt_ps[:].rearrange("w t u c -> w t c u"),
-                )
+        def live(n):
+            return 0 <= n < HEADS
+
+        def transpose_x(m):
+            if not live(m):
+                return
+            b, pair = m // 2, m % 2
+            if pair == 0:
+                x_grouped = work.tile([P, PACK * S], BF16, align_bytes=64)
+                x_grouped_of[b] = x_grouped
+            x_words = x_grouped_of[b][:].bitcast(F32).rearrange("w (t c u) -> w t c u", t=PACK, u=2)
+            xt_ps = psum.tile([P, 2, 2, P], F32, tag="bank")
+            for tl in range(2):
+                t = 2 * pair + tl
+                row = 2 * (t % 2) + t // 2
+                for u in range(2):
+                    nc.tensor.transpose(
+                        out=xt_ps[:, tl, u, :],
+                        in_=x_rows[b][:, row, :].bitcast(F32)[:, P * u : P * (u + 1)],
+                        identity=ident_f32[:],
+                    )
+            nc.vector.tensor_copy(
+                out=x_words[:, 2 * pair : 2 * pair + 2], in_=xt_ps[:].rearrange("w t u c -> w t c u")
+            )
+
+        def quantise_x(m):
+            if not live(m) or m % 2 == 0:
+                return
+            b = m // 2
             x_codes = work.tile([P, S], U32, align_bytes=64)
             x_scales = work.tile([P, S], U8, align_bytes=64)
-            nc.vector.quantize_mx(out=x_codes[:].bitcast(FP8X4), scales=x_scales[:], in_=x_grouped[:])
+            nc.vector.quantize_mx(
+                out=x_codes[:].bitcast(FP8X4), scales=x_scales[:], in_=x_grouped_of[b][:]
+            )
             x_mx[b] = (x_codes, x_scales)
 
-        def project_v(b):
+        def project_v(m):
+            if not live(m):
+                return
+            b = m // 2
             x_codes, x_scales = x_mx[b]
-            v_grouped = work.tile([P, D, PACK], BF16, align_bytes=64)
-            for c in range(D // P):
+            if m % 2 == 0:
+                v_grouped = work.tile([P, D, PACK], BF16, align_bytes=64)
+                v_grouped_of[b] = v_grouped
+            for c in (2 * (m % 2), 2 * (m % 2) + 1):
                 cols = slice(P * c, P * (c + 1))
-                v_ps = psum.tile([P, PACK, P], F32, tag="prep", bufs=2)
+                v_ps = psum.tile([P, PACK, P], F32, tag="bank")
                 for t in range(PACK):
                     keys = slice(P * t, P * (t + 1))
                     nc.tensor.matmul_mx(
@@ -140,156 +162,188 @@ def tile_selfattention_pa_t_kernel(tc, x, Wv, bv, q, k, out):
                         stop=True,
                     )
                 nc.vector.tensor_tensor(
-                    out=v_grouped[:, cols, :],
+                    out=v_grouped_of[b][:, cols, :],
                     in0=v_ps[:].rearrange("p t n -> p n t"),
                     in1=bv_all[:, cols].unsqueeze(2).to_broadcast([P, P, PACK]),
                     op=ALU.add,
                 )
-            v_codes = work.tile([P, D], U32, align_bytes=64, bufs=3)
-            v_scales = work.tile([P, D], U8, align_bytes=64, bufs=3)
+
+        def quantise_v(m):
+            if not live(m) or m % 2 == 0:
+                return
+            b = m // 2
+            v_codes = work.tile([P, D], U32, align_bytes=64)
+            v_scales = work.tile([P, D], U8, align_bytes=64)
             nc.vector.quantize_mx(
                 out=v_codes[:].bitcast(FP8X4),
                 scales=v_scales[:],
-                in_=v_grouped[:].rearrange("p n t -> p (n t)"),
+                in_=v_grouped_of[b][:].rearrange("p n t -> p (n t)"),
             )
             v_mx[b] = (v_codes, v_scales)
 
-        def prepare_qk(n):
-            b, h = n // H, n % H
-            qt_ps = psum.tile([P, Q_TILES, P], F32, tag="prep", bufs=2)
+        def transpose_q(n):
+            if not live(n):
+                return
+            qt_ps = psum.tile([P, Q_TILES, P], F32, tag="bank")
             for it in range(Q_TILES):
                 nc.tensor.transpose(
-                    out=qt_ps[:, it, :], in_=q_rows[b][:, h, it, :].bitcast(F32), identity=ident_f32[:]
+                    out=qt_ps[:, it, :], in_=q_rows[n][:, it, :].bitcast(F32), identity=ident_f32[:]
                 )
             q_t = work.tile([P, 2 * S], BF16, bufs=3)
-            nc.scalar.copy(out=q_t[:], in_=qt_ps[:].rearrange("w a i -> w (a i)").bitcast(BF16))
-            kt_ps = psum.tile([P, 2, 2, P], F32, tag="prep", bufs=2)
+            nc.scalar.copy(out=q_t[:].bitcast(F32), in_=qt_ps[:].rearrange("w a i -> w (a i)"))
+            q_t_of[n] = q_t
+
+        def transpose_k(n):
+            if not live(n):
+                return
+            kt_ps = psum.tile([P, 2, 2, P], F32, tag="bank")
             for u in range(2):
                 for half in range(2):
                     nc.tensor.transpose(
                         out=kt_ps[:, u, half, :],
-                        in_=k_rows[b][:, h, half, u, :].bitcast(F32),
+                        in_=k_rows[n][:, half, u, :].bitcast(F32),
                         identity=ident_f32[:],
                     )
             k_t = work.tile([P, 2 * S], BF16, bufs=3)
-            nc.scalar.copy(out=k_t[:], in_=kt_ps[:].rearrange("w u a r -> w (u a r)").bitcast(BF16))
-            qk_t[n] = (q_t, k_t)
+            nc.scalar.copy(out=k_t[:].bitcast(F32), in_=kt_ps[:].rearrange("w u a r -> w (u a r)"))
+            k_t_of[n] = k_t
 
-        def attend(n):
-            h = n % H
-            q_t, k_t = qk_t[n]
-            q_view = q_t[:].rearrange("w (a i e) -> w a i e", a=Q_TILES, e=2)
-            k_view = k_t[:].rearrange("w (u c e) -> w u c e", u=2, e=2)
-            bias_view = bias_of_head[h][:].rearrange("i (u c) -> i u c", u=2)
-            e_sb = e_tiles[n % E_COPIES]
-            row_sum = small.tile([P, Q_TILES], F32)
-            for it in range(Q_TILES):
-                width = (P // 2) * (it + 1)
-                s_ps = psum.tile([P, S], F32, tag="scores", bufs=3)
-                s_view = s_ps[:, : 2 * width].rearrange("i (u c) -> i u c", u=2)
-                for e in range(2):
-                    nc.tensor.matmul(
-                        out=s_view,
-                        lhsT=q_view[:, it, :, e],
-                        rhs=k_view[:, :, :width, e],
-                        start=(e == 0),
-                        stop=False,
-                    )
+        def score_tile(n, it):
+            if not live(n):
+                return
+            q_view = q_t_of[n][:].rearrange("w (a i e) -> w a i e", a=Q_TILES, e=2)
+            k_view = k_t_of[n][:].rearrange("w (u c e) -> w u c e", u=2, e=2)
+            bias_view = bias_of_head[n % H][:].rearrange("i (u c) -> i u c", u=2)
+            width = (P // 2) * (it + 1)
+            s_ps = psum.tile([P, S], F32, tag="bank")
+            s_view = s_ps[:, : 2 * width].rearrange("i (u c) -> i u c", u=2)
+            for e in range(2):
                 nc.tensor.matmul(
                     out=s_view,
-                    lhsT=ident_bf16[:],
-                    rhs=bias_view[:, :, S // 2 - width :],
-                    start=False,
-                    stop=True,
+                    lhsT=q_view[:, it, :, e],
+                    rhs=k_view[:, :, :width, e],
+                    start=(e == 0),
+                    stop=False,
                 )
-                unread = small.tile([P, S], BF16)
-                neg_max = small.tile([P, 1], F32)
-                nc.vector.tensor_scalar(
-                    out=unread[:, : 2 * width],
-                    in0=s_ps[:, : 2 * width],
-                    scalar1=-SCORE_SCALE,
-                    scalar2=None,
-                    op0=ALU.mult,
-                    op1=ALU.min,
-                    accum_out=neg_max[:],
-                )
-                nc.scalar.activation(
-                    out=e_sb[:, it, :, :width],
-                    in_=s_view,
-                    func=ACT.Exp,
-                    bias=neg_max[:],
-                    scale=SCORE_SCALE,
-                    accum_out=row_sum[:, it : it + 1],
-                )
-            e_of[n] = e_sb
-            sums[n] = row_sum
+            nc.tensor.matmul(
+                out=s_view,
+                lhsT=ident_bf16[:],
+                rhs=bias_view[:, :, S // 2 - width :],
+                start=False,
+                stop=True,
+            )
+            unread = small.tile([P, S], BF16)
+            neg_max = small.tile([P, 1], F32)
+            nc.vector.tensor_scalar(
+                out=unread[:, : 2 * width],
+                in0=s_ps[:, : 2 * width],
+                scalar1=-SCORE_SCALE,
+                scalar2=None,
+                op0=ALU.mult,
+                op1=ALU.min,
+                accum_out=neg_max[:],
+            )
+            s_of[(n, it)] = s_view
+            neg_max_of[(n, it)] = neg_max
 
-        def transpose_e(n):
-            e_sb = e_of[n]
-            e_grouped = work.tile([P, PACK * S], BF16, align_bytes=64)
-            e_words = e_grouped[:].bitcast(F32).rearrange("p (a i u) -> p a i u", a=Q_TILES, u=2)
-            for pair in range(Q_TILES // 2):
-                et_ps = psum.tile([P, 2, 2, P], F32, tag="tail", bufs=3)
-                for a in range(2):
-                    for u in range(2):
-                        nc.tensor.transpose(
-                            out=et_ps[:, a, u, :],
-                            in_=e_sb[:, 2 * pair + a, u, :].bitcast(F32),
-                            identity=ident_f32[:],
-                        )
-                nc.scalar.copy(
-                    out=e_words[:, 2 * pair : 2 * pair + 2],
-                    in_=et_ps[:].rearrange("p a u i -> p a i u"),
-                )
+        def exponential(n, it):
+            if not live(n):
+                return
+            if n not in sums:
+                row_sum = small.tile([P, Q_TILES], F32)
+                sums[n] = row_sum
+            width = (P // 2) * (it + 1)
+            nc.scalar.activation(
+                out=e_tiles[n % E_COPIES][:, it, :, :width],
+                in_=s_of[(n, it)],
+                func=ACT.Exp,
+                bias=neg_max_of[(n, it)][:],
+                scale=SCORE_SCALE,
+                accum_out=sums[n][:, it : it + 1],
+            )
+
+        def transpose_e(n, pair):
+            if not live(n):
+                return
+            if pair == 0:
+                e_grouped = work.tile([P, PACK * S], BF16, align_bytes=64)
+                e_grouped_of[n] = e_grouped
+            e_words = e_grouped_of[n][:].bitcast(F32).rearrange("p (a i u) -> p a i u", a=Q_TILES, u=2)
+            et_ps = psum.tile([P, 2, 2, P], F32, tag="bank")
+            for a in range(2):
+                for u in range(2):
+                    nc.tensor.transpose(
+                        out=et_ps[:, a, u, :],
+                        in_=e_tiles[n % E_COPIES][:, 2 * pair + a, u, :].bitcast(F32),
+                        identity=ident_f32[:],
+                    )
+            nc.scalar.copy(
+                out=e_words[:, 2 * pair : 2 * pair + 2], in_=et_ps[:].rearrange("p a u i -> p a i u")
+            )
+
+        def quantise_e(n):
+            if not live(n):
+                return
             e_codes = work.tile([P, S], U32, align_bytes=64)
             e_scales = work.tile([P, S], U8, align_bytes=64)
-            nc.vector.quantize_mx(out=e_codes[:].bitcast(FP8X4), scales=e_scales[:], in_=e_grouped[:])
+            nc.vector.quantize_mx(
+                out=e_codes[:].bitcast(FP8X4), scales=e_scales[:], in_=e_grouped_of[n][:]
+            )
             e_mx[n] = (e_codes, e_scales)
 
-        def context(n):
+        def context(n, pair):
+            if not live(n):
+                return
             b, h = n // H, n % H
             e_codes, e_scales = e_mx[n]
             v_codes, v_scales = v_mx[b]
             dims = slice(HD * h, HD * (h + 1))
-            inv_sum = small.tile([P, Q_TILES], F32)
-            nc.vector.reciprocal(out=inv_sum[:], in_=sums[n][:])
-            ctx_sb = work.tile([P, Q_TILES, HD], F32, bufs=4)
-            for pair in range(Q_TILES // 2):
-                c_ps = psum.tile([P, 2, HD], F32, tag="tail", bufs=3)
-                for a in range(2):
-                    queries = slice(P * (2 * pair + a), P * (2 * pair + a + 1))
-                    nc.tensor.matmul_mx(
-                        out=c_ps[:, a, :],
-                        lhsT=e_codes[:, queries].bitcast(FP8X4),
-                        lhsT_scale=e_scales[:, queries],
-                        rhs=v_codes[:, dims].bitcast(FP8X4),
-                        rhs_scale=v_scales[:, dims],
-                        start=True,
-                        stop=True,
-                    )
-                for a in range(2):
-                    it = 2 * pair + a
-                    nc.scalar.activation(
-                        out=ctx_sb[:, it, :], in_=c_ps[:, a, :], func=ACT.Copy, scale=inv_sum[:, it : it + 1]
-                    )
-            nc.sync.dma_start(
-                out=out[b, :, dims].rearrange("(it p) d -> p it d", p=P), in_=ctx_sb[:]
-            )
+            if pair == 0:
+                inv_sum = small.tile([P, Q_TILES], F32)
+                nc.vector.reciprocal(out=inv_sum[:], in_=sums[n][:])
+                inv_of[n] = inv_sum
+                ctx_sb = work.tile([P, Q_TILES, HD], F32, bufs=4)
+                ctx_of[n] = ctx_sb
+            c_ps = psum.tile([P, 2, HD], F32, tag="bank")
+            for a in range(2):
+                queries = slice(P * (2 * pair + a), P * (2 * pair + a + 1))
+                nc.tensor.matmul_mx(
+                    out=c_ps[:, a, :],
+                    lhsT=e_codes[:, queries].bitcast(FP8X4),
+                    lhsT_scale=e_scales[:, queries],
+                    rhs=v_codes[:, dims].bitcast(FP8X4),
+                    rhs_scale=v_scales[:, dims],
+                    start=True,
+                    stop=True,
+                )
+            for a in range(2):
+                it = 2 * pair + a
+                nc.scalar.activation(
+                    out=ctx_of[n][:, it, :], in_=c_ps[:, a, :], func=ACT.Copy, scale=inv_of[n][:, it : it + 1]
+                )
+            if pair == 1:
+                nc.sync.dma_start(
+                    out=out[b, :, dims].rearrange("(it p) d -> p it d", p=P), in_=ctx_of[n][:]
+                )
 
-        prepare_qk(0)
-        prepare_x(0)
-        prepare_qk(1)
-        project_v(0)
-        for n in range(HEADS + 2):
-            if n < HEADS:
-                attend(n)
-            if 1 <= n <= HEADS:
-                transpose_e(n - 1)
-            if n + 2 < HEADS:
-                prepare_qk(n + 2)
-            if n % 2 == 0 and n // 2 + 1 < B:
-                prepare_x(n // 2 + 1)
-            if n >= 2:
-                context(n - 2)
-            if n % 2 == 1 and n // 2 + 1 < B:
-                project_v(n // 2 + 1)
+        ctx.enter_context(tc.manual_schedule())
+        for n in range(-3, HEADS + 2):
+            score_tile(n, 3)
+            transpose_e(n - 1, 0)
+            exponential(n, 3)
+            quantise_e(n - 2)
+            score_tile(n, 2)
+            transpose_e(n - 1, 1)
+            exponential(n, 2)
+            score_tile(n, 1)
+            exponential(n, 1)
+            transpose_q(n + 2)
+            score_tile(n, 0)
+            exponential(n, 0)
+            transpose_k(n + 2)
+            quantise_v(n)
+            transpose_x(n + 3)
+            quantise_x(n + 3)
+            context(n - 2, 0)
+            context(n - 2, 1)
+            project_v(n + 1)

@@ -33,38 +33,52 @@ def tile_selfattention_pa_t_kernel(tc, x, Wv, bv, q, k, out):
         const = ctx.enter_context(tc.tile_pool(name="const", bufs=1))
         loads = ctx.enter_context(tc.tile_pool(name="loads", bufs=HEADS))
         work = ctx.enter_context(tc.tile_pool(name="work", bufs=2))
-        small = ctx.enter_context(tc.tile_pool(name="small", bufs=6))
+        small = ctx.enter_context(tc.tile_pool(name="small", bufs=8))
         psum = ctx.enter_context(tc.psum_pool(name="psum", bufs=PSUM_BANKS))
+        ctx.enter_context(tc.manual_schedule())
 
         wv_raw = const.tile([P, PACK, D], BF16)
-        nc.scalar.dma_start(
-            out=wv_raw[:].rearrange("w (u e) n -> w u e n", u=2),
-            in_=Wv.rearrange("(u w e) n -> w u e n", u=2, e=2),
-        )
+        x_rows, q_rows, k_rows = [], [], []
+        for n in range(HEADS):
+            b, h = n // H, n % H
+            q_sb = loads.tile([P, Q_TILES, HD], BF16)
+            nc.sync.dma_start(out=q_sb[:], in_=q[b, h].rearrange("(it p) d -> p it d", p=P))
+            q_rows.append(q_sb)
+            k_sb = loads.tile([P, 2, 2, HD], BF16)
+            nc.sync.dma_start(
+                out=k_sb[:], in_=k[b, h].rearrange("(half r u) d -> r half u d", half=2, u=2)
+            )
+            k_rows.append(k_sb)
+            if n == 0:
+                nc.sync.dma_start(
+                    out=wv_raw[:].rearrange("w (u e) n -> w u e n", u=2),
+                    in_=Wv.rearrange("(u w e) n -> w u e n", u=2, e=2),
+                )
+            if h == 0:
+                x_sb = loads.tile([P, PACK, D], BF16, bufs=B)
+                nc.sync.dma_start(out=x_sb[:], in_=x[b].rearrange("(p t) f -> p t f", t=PACK))
+                x_rows.append(x_sb)
         bv_all = const.tile([P, D], BF16)
         nc.scalar.dma_start(out=bv_all[:], in_=bv.partition_broadcast(P))
-        x_rows, q_rows, k_rows = [], [], []
-        for b in range(B):
-            x_sb = loads.tile([P, PACK, D], BF16, bufs=B)
-            nc.sync.dma_start(out=x_sb[:], in_=x[b].rearrange("(p t) f -> p t f", t=PACK))
-            x_rows.append(x_sb)
-            for h in range(H):
-                q_sb = loads.tile([P, Q_TILES, HD], BF16)
-                nc.sync.dma_start(out=q_sb[:], in_=q[b, h].rearrange("(it p) d -> p it d", p=P))
-                q_rows.append(q_sb)
-                k_sb = loads.tile([P, 2, 2, HD], BF16)
-                nc.sync.dma_start(
-                    out=k_sb[:], in_=k[b, h].rearrange("(half r u) d -> r half u d", half=2, u=2)
-                )
-                k_rows.append(k_sb)
 
+        key_pos = const.tile([P, S], I32)
+        nc.gpsimd.iota(key_pos[:], pattern=[[1, 2], [4, P], [2, 2]], base=-(S // 2), channel_multiplier=0)
         ident_f32 = const.tile([P, P], F32)
         make_identity(nc, ident_f32[:])
         ident_bf16 = const.tile([P, P], BF16)
         make_identity(nc, ident_bf16[:])
 
-        key_pos = const.tile([P, S], I32)
-        nc.gpsimd.iota(key_pos[:], pattern=[[1, 2], [4, P], [2, 2]], base=-(S // 2), channel_multiplier=0)
+        zero = const.tile([P, 1], F32)
+        nc.vector.memset(zero[:], 0.0)
+        one = const.tile([P, 1], F32)
+        nc.scalar.activation(out=one[:], in_=zero[:], func=ACT.Exp)
+
+        e_tiles = []
+        for i in range(E_COPIES):
+            e_sb = const.tile([P, Q_TILES, 2, S // 2], BF16, name="e_sb_%d" % i)
+            nc.vector.memset(e_sb[:], 0.0)
+            e_tiles.append(e_sb)
+
         bias_f32 = const.tile([P, S], F32)
         nc.vector.tensor_copy(out=bias_f32[:], in_=key_pos[:])
         nc.gpsimd.affine_select(
@@ -83,12 +97,6 @@ def tile_selfattention_pa_t_kernel(tc, x, Wv, bv, q, k, out):
             nc.vector.tensor_scalar_mul(out=bias_bf16[:], in0=bias_f32[:], scalar1=slope / SCORE_SCALE)
             bias_of_head.append(bias_bf16)
 
-        e_tiles = []
-        for i in range(E_COPIES):
-            e_sb = const.tile([P, Q_TILES, 2, S // 2], BF16, name="e_sb_%d" % i)
-            nc.vector.memset(e_sb[:], 0.0)
-            e_tiles.append(e_sb)
-
         wv_grouped = const.tile([P, D, PACK], BF16, align_bytes=64)
         nc.vector.tensor_copy(out=wv_grouped[:], in_=wv_raw[:].rearrange("w t n -> w n t"))
         wv_codes = const.tile([P, D], U32, align_bytes=64)
@@ -101,7 +109,7 @@ def tile_selfattention_pa_t_kernel(tc, x, Wv, bv, q, k, out):
 
         x_grouped_of, x_mx, v_grouped_of, v_mx = {}, {}, {}, {}
         q_t_of, k_t_of, s_of, neg_max_of, sums = {}, {}, {}, {}, {}
-        e_grouped_of, e_mx, inv_of, ctx_of = {}, {}, {}, {}
+        e_grouped_of, e_mx, inv_of = {}, {}, {}
 
         def live(n):
             return 0 <= n < HEADS
@@ -139,34 +147,33 @@ def tile_selfattention_pa_t_kernel(tc, x, Wv, bv, q, k, out):
             )
             x_mx[b] = (x_codes, x_scales)
 
-        def project_v(m):
+        def project_v(m, j):
             if not live(m):
                 return
-            b = m // 2
+            b, c = m // 2, 2 * (m % 2) + j
             x_codes, x_scales = x_mx[b]
-            if m % 2 == 0:
+            if c == 0:
                 v_grouped = work.tile([P, D, PACK], BF16, align_bytes=64)
                 v_grouped_of[b] = v_grouped
-            for c in (2 * (m % 2), 2 * (m % 2) + 1):
-                cols = slice(P * c, P * (c + 1))
-                v_ps = psum.tile([P, PACK, P], F32, tag="bank")
-                for t in range(PACK):
-                    keys = slice(P * t, P * (t + 1))
-                    nc.tensor.matmul_mx(
-                        out=v_ps[:, t, :],
-                        lhsT=x_codes[:, keys].bitcast(FP8X4),
-                        lhsT_scale=x_scales[:, keys],
-                        rhs=wv_codes[:, cols].bitcast(FP8X4),
-                        rhs_scale=wv_scales[:, cols],
-                        start=True,
-                        stop=True,
-                    )
-                nc.vector.tensor_tensor(
-                    out=v_grouped_of[b][:, cols, :],
-                    in0=v_ps[:].rearrange("p t n -> p n t"),
-                    in1=bv_all[:, cols].unsqueeze(2).to_broadcast([P, P, PACK]),
-                    op=ALU.add,
+            cols = slice(P * c, P * (c + 1))
+            v_ps = psum.tile([P, PACK, P], F32, tag="bank")
+            for t in range(PACK):
+                keys = slice(P * t, P * (t + 1))
+                nc.tensor.matmul_mx(
+                    out=v_ps[:, t, :],
+                    lhsT=x_codes[:, keys].bitcast(FP8X4),
+                    lhsT_scale=x_scales[:, keys],
+                    rhs=wv_codes[:, cols].bitcast(FP8X4),
+                    rhs_scale=wv_scales[:, cols],
+                    start=True,
+                    stop=True,
                 )
+            nc.vector.tensor_tensor(
+                out=v_grouped_of[b][:, cols, :],
+                in0=v_ps[:].rearrange("p t n -> p n t"),
+                in1=bv_all[:, cols].unsqueeze(2).to_broadcast([P, P, PACK]),
+                op=ALU.add,
+            )
 
         def quantise_v(m):
             if not live(m) or m % 2 == 0:
@@ -232,10 +239,10 @@ def tile_selfattention_pa_t_kernel(tc, x, Wv, bv, q, k, out):
                 start=False,
                 stop=True,
             )
-            unread = small.tile([P, S], BF16)
+            neg_s = small.tile([P, S], F32)
             neg_max = small.tile([P, 1], F32)
             nc.vector.tensor_scalar(
-                out=unread[:, : 2 * width],
+                out=neg_s[:, : 2 * width],
                 in0=s_ps[:, : 2 * width],
                 scalar1=-SCORE_SCALE,
                 scalar2=None,
@@ -243,7 +250,7 @@ def tile_selfattention_pa_t_kernel(tc, x, Wv, bv, q, k, out):
                 op1=ALU.min,
                 accum_out=neg_max[:],
             )
-            s_of[(n, it)] = s_view
+            s_of[(n, it)] = neg_s
             neg_max_of[(n, it)] = neg_max
 
         def exponential(n, it):
@@ -255,20 +262,18 @@ def tile_selfattention_pa_t_kernel(tc, x, Wv, bv, q, k, out):
             width = (P // 2) * (it + 1)
             nc.scalar.activation(
                 out=e_tiles[n % E_COPIES][:, it, :, :width],
-                in_=s_of[(n, it)],
+                in_=s_of[(n, it)][:, : 2 * width].rearrange("i (u c) -> i u c", u=2),
                 func=ACT.Exp,
                 bias=neg_max_of[(n, it)][:],
-                scale=SCORE_SCALE,
+                scale=-1.0,
                 accum_out=sums[n][:, it : it + 1],
             )
 
         def transpose_e(n, pair):
             if not live(n):
                 return
-            if pair == 0:
-                e_grouped = work.tile([P, PACK * S], BF16, align_bytes=64)
-                e_grouped_of[n] = e_grouped
-            e_words = e_grouped_of[n][:].bitcast(F32).rearrange("p (a i u) -> p a i u", a=Q_TILES, u=2)
+            e_grouped = work.tile([P, 2 * S], BF16, align_bytes=64, bufs=4)
+            e_grouped_of[(n, pair)] = e_grouped
             et_ps = psum.tile([P, 2, 2, P], F32, tag="bank")
             for a in range(2):
                 for u in range(2):
@@ -278,35 +283,34 @@ def tile_selfattention_pa_t_kernel(tc, x, Wv, bv, q, k, out):
                         identity=ident_f32[:],
                     )
             nc.scalar.copy(
-                out=e_words[:, 2 * pair : 2 * pair + 2], in_=et_ps[:].rearrange("p a u i -> p a i u")
+                out=e_grouped[:].bitcast(F32).rearrange("p (a i u) -> p a i u", a=2, u=2),
+                in_=et_ps[:].rearrange("p a u i -> p a i u"),
             )
 
-        def quantise_e(n):
+        def quantise_e(n, pair):
             if not live(n):
                 return
-            e_codes = work.tile([P, S], U32, align_bytes=64)
-            e_scales = work.tile([P, S], U8, align_bytes=64)
+            e_codes = work.tile([P, S // 2], U32, align_bytes=64, bufs=4)
+            e_scales = work.tile([P, S // 2], U8, align_bytes=64, bufs=4)
             nc.vector.quantize_mx(
-                out=e_codes[:].bitcast(FP8X4), scales=e_scales[:], in_=e_grouped_of[n][:]
+                out=e_codes[:].bitcast(FP8X4), scales=e_scales[:], in_=e_grouped_of[(n, pair)][:]
             )
-            e_mx[n] = (e_codes, e_scales)
+            e_mx[(n, pair)] = (e_codes, e_scales)
 
         def context(n, pair):
             if not live(n):
                 return
             b, h = n // H, n % H
-            e_codes, e_scales = e_mx[n]
+            e_codes, e_scales = e_mx[(n, pair)]
             v_codes, v_scales = v_mx[b]
             dims = slice(HD * h, HD * (h + 1))
-            if pair == 0:
+            if n not in inv_of:
                 inv_sum = small.tile([P, Q_TILES], F32)
                 nc.vector.reciprocal(out=inv_sum[:], in_=sums[n][:])
                 inv_of[n] = inv_sum
-                ctx_sb = work.tile([P, Q_TILES, HD], F32, bufs=4)
-                ctx_of[n] = ctx_sb
             c_ps = psum.tile([P, 2, HD], F32, tag="bank")
             for a in range(2):
-                queries = slice(P * (2 * pair + a), P * (2 * pair + a + 1))
+                queries = slice(P * a, P * (a + 1))
                 nc.tensor.matmul_mx(
                     out=c_ps[:, a, :],
                     lhsT=e_codes[:, queries].bitcast(FP8X4),
@@ -316,34 +320,34 @@ def tile_selfattention_pa_t_kernel(tc, x, Wv, bv, q, k, out):
                     start=True,
                     stop=True,
                 )
+            ctx_sb = work.tile([P, 2, HD], F32, bufs=6)
             for a in range(2):
                 it = 2 * pair + a
                 nc.scalar.activation(
-                    out=ctx_of[n][:, it, :], in_=c_ps[:, a, :], func=ACT.Copy, scale=inv_of[n][:, it : it + 1]
+                    out=ctx_sb[:, a, :], in_=c_ps[:, a, :], func=ACT.Copy, scale=inv_of[n][:, it : it + 1]
                 )
-            if pair == 1:
-                nc.sync.dma_start(
-                    out=out[b, :, dims].rearrange("(it p) d -> p it d", p=P), in_=ctx_of[n][:]
-                )
+            rows = slice(2 * P * pair, 2 * P * (pair + 1))
+            nc.sync.dma_start(out=out[b, rows, dims].rearrange("(a p) d -> p a d", p=P), in_=ctx_sb[:])
 
-        ctx.enter_context(tc.manual_schedule())
-        for n in range(-3, HEADS + 2):
+        for n in range(-2, HEADS + 3):
             score_tile(n, 3)
-            transpose_e(n - 1, 0)
-            exponential(n, 3)
-            quantise_e(n - 2)
             score_tile(n, 2)
             transpose_e(n - 1, 1)
-            exponential(n, 2)
+            exponential(n, 3)
+            quantise_e(n - 2, 1)
+            quantise_e(n - 2, 0)
             score_tile(n, 1)
-            exponential(n, 1)
-            transpose_q(n + 2)
             score_tile(n, 0)
-            exponential(n, 0)
+            transpose_e(n - 1, 0)
+            exponential(n, 2)
+            transpose_q(n + 2)
+            exponential(n, 1)
             transpose_k(n + 2)
-            quantise_v(n)
-            transpose_x(n + 3)
-            quantise_x(n + 3)
-            context(n - 2, 0)
-            context(n - 2, 1)
-            project_v(n + 1)
+            exponential(n, 0)
+            quantise_v(n - 1)
+            transpose_x(n + 2)
+            quantise_x(n + 2)
+            context(n - 3, 1)
+            project_v(n, 0)
+            context(n - 3, 0)
+            project_v(n, 1)

@@ -6,7 +6,6 @@ from concourse.masks import make_identity
 
 F32 = mybir.dt.float32
 BF16 = mybir.dt.bfloat16
-I32 = mybir.dt.int32
 U32 = mybir.dt.uint32
 U8 = mybir.dt.uint8
 FP8X4 = mybir.dt.float8_e4m3fn_x4
@@ -61,12 +60,26 @@ def tile_selfattention_pa_t_kernel(tc, x, Wv, bv, q, k, out):
         bv_all = const.tile([P, D], BF16)
         nc.scalar.dma_start(out=bv_all[:], in_=bv.partition_broadcast(P))
 
-        key_pos = const.tile([P, S], I32)
-        nc.gpsimd.iota(key_pos[:], pattern=[[1, 2], [4, P], [2, 2]], base=-(S // 2), channel_multiplier=0)
         ident_f32 = const.tile([P, P], F32)
         make_identity(nc, ident_f32[:])
-        ident_bf16 = const.tile([P, P], BF16)
-        make_identity(nc, ident_bf16[:])
+        bias_f32 = const.tile([P, S], F32)
+        nc.gpsimd.iota(
+            bias_f32[:],
+            pattern=[[1, 2], [4, P], [2, 2]],
+            base=-(S // 2),
+            channel_multiplier=0,
+            allow_small_or_imprecise_dtypes=True,
+        )
+        diagonal = bias_f32[:].rearrange("i (u c) -> i u c", u=2)[:, :, (S - P) // 2 :]
+        nc.gpsimd.affine_select(
+            out=diagonal,
+            in_=diagonal,
+            pattern=[[-1, 2], [-4, P // PACK], [-2, 2]],
+            compare_op=ALU.is_ge,
+            fill=MASKED,
+            base=0,
+            channel_multiplier=1,
+        )
 
         zero = const.tile([P, 1], F32)
         nc.vector.memset(zero[:], 0.0)
@@ -79,17 +92,8 @@ def tile_selfattention_pa_t_kernel(tc, x, Wv, bv, q, k, out):
             nc.vector.memset(e_sb[:], 0.0)
             e_tiles.append(e_sb)
 
-        bias_f32 = const.tile([P, S], F32)
-        nc.vector.tensor_copy(out=bias_f32[:], in_=key_pos[:])
-        nc.gpsimd.affine_select(
-            out=bias_f32[:],
-            in_=bias_f32[:],
-            pattern=[[-1, 2], [-4, P], [-2, 2]],
-            compare_op=ALU.is_ge,
-            fill=MASKED,
-            base=S - P,
-            channel_multiplier=1,
-        )
+        ident_bf16 = const.tile([P, P], BF16)
+        nc.vector.tensor_copy(out=ident_bf16[:], in_=ident_f32[:])
         bias_of_head = []
         for h in range(H):
             slope = 2.0 ** (-8.0 / H * (h + 1))

@@ -36,6 +36,11 @@ def tile_selfattention_pa_t_kernel(tc, x, Wv, bv, q, k, out):
         psum = ctx.enter_context(tc.psum_pool(name="psum", bufs=PSUM_BANKS))
         ctx.enter_context(tc.manual_schedule())
 
+        bv_row = const.tile([P, D], BF16)
+        nc.vector.memset(bv_row[:], 0.0)
+        ones = const.tile([P, P], BF16)
+        nc.vector.memset(ones[:], 1.0)
+
         wv_raw = const.tile([P, PACK, D], BF16)
         x_rows, q_rows, k_rows = [], [], []
         for n in range(HEADS):
@@ -57,8 +62,8 @@ def tile_selfattention_pa_t_kernel(tc, x, Wv, bv, q, k, out):
                 x_sb = loads.tile([P, PACK, D], BF16, bufs=B)
                 nc.sync.dma_start(out=x_sb[:], in_=x[b].rearrange("(p t) f -> p t f", t=PACK))
                 x_rows.append(x_sb)
-        bv_all = const.tile([P, D], BF16)
-        nc.scalar.dma_start(out=bv_all[:], in_=bv.partition_broadcast(P))
+            if n == 0:
+                nc.sync.dma_start(out=bv_row[0:1, :], in_=bv.rearrange("(o n) -> o n", o=1))
 
         ident_f32 = const.tile([P, P], F32)
         make_identity(nc, ident_f32[:])
@@ -117,6 +122,13 @@ def tile_selfattention_pa_t_kernel(tc, x, Wv, bv, q, k, out):
 
         def live(n):
             return 0 <= n < HEADS
+
+        bv_all = const.tile([P, D], BF16)
+
+        def spread_bv():
+            bv_ps = psum.tile([P, D], F32, tag="bank")
+            nc.tensor.matmul(out=bv_ps[:], lhsT=ones[:], rhs=bv_row[:], start=True, stop=True)
+            nc.vector.tensor_copy(out=bv_all[:], in_=bv_ps[:])
 
         def transpose_x(m):
             if not live(m):
@@ -355,3 +367,5 @@ def tile_selfattention_pa_t_kernel(tc, x, Wv, bv, q, k, out):
             project_v(n, 0)
             context(n - 3, 0)
             project_v(n, 1)
+            if n == -2:
+                spread_bv()

@@ -22,6 +22,7 @@ SCORE_SCALE = 1.0 / math.sqrt(HD)
 MASKED = -3.0e38
 E_COPIES = 3
 PSUM_BANKS = 8
+ROTATING_BANKS = PSUM_BANKS - 1
 
 FLOPS = 2 * B * S * D * D + 2 * (2 * B * H * S * S * HD)
 
@@ -33,7 +34,8 @@ def tile_selfattention_pa_t_kernel(tc, x, Wv, bv, q, k, out):
         loads = ctx.enter_context(tc.tile_pool(name="loads", bufs=HEADS))
         work = ctx.enter_context(tc.tile_pool(name="work", bufs=2))
         small = ctx.enter_context(tc.tile_pool(name="small", bufs=8))
-        psum = ctx.enter_context(tc.psum_pool(name="psum", bufs=PSUM_BANKS))
+        psum = ctx.enter_context(tc.psum_pool(name="psum", bufs=ROTATING_BANKS))
+        psum_fixed = ctx.enter_context(tc.psum_pool(name="psum_fixed", bufs=1))
         ctx.enter_context(tc.manual_schedule())
 
         bv_row = const.tile([P, D], BF16)
@@ -60,7 +62,10 @@ def tile_selfattention_pa_t_kernel(tc, x, Wv, bv, q, k, out):
                 )
             if h == 0:
                 x_sb = loads.tile([P, PACK, D], BF16, bufs=B)
-                nc.sync.dma_start(out=x_sb[:], in_=x[b].rearrange("(p t) f -> p t f", t=PACK))
+                nc.sync.dma_start(
+                    out=x_sb[:].rearrange("p (u e) f -> p u e f", u=2),
+                    in_=x[b].rearrange("(u p e) f -> p u e f", u=2, e=2),
+                )
                 x_rows.append(x_sb)
             if n == 0:
                 nc.sync.dma_start(out=bv_row[0:1, :], in_=bv.rearrange("(o n) -> o n", o=1))
@@ -70,16 +75,16 @@ def tile_selfattention_pa_t_kernel(tc, x, Wv, bv, q, k, out):
         bias_f32 = const.tile([P, S], F32)
         nc.gpsimd.iota(
             bias_f32[:],
-            pattern=[[1, 2], [4, P], [2, 2]],
+            pattern=[[1, S]],
             base=-(S // 2),
             channel_multiplier=0,
             allow_small_or_imprecise_dtypes=True,
         )
-        diagonal = bias_f32[:].rearrange("i (u c) -> i u c", u=2)[:, :, (S - P) // 2 :]
+        diagonal = bias_f32[:, S - P :]
         nc.gpsimd.affine_select(
             out=diagonal,
             in_=diagonal,
-            pattern=[[-1, 2], [-4, P // PACK], [-2, 2]],
+            pattern=[[-1, P]],
             compare_op=ALU.is_ge,
             fill=MASKED,
             base=0,
@@ -93,12 +98,18 @@ def tile_selfattention_pa_t_kernel(tc, x, Wv, bv, q, k, out):
 
         e_tiles = []
         for i in range(E_COPIES):
-            e_sb = const.tile([P, Q_TILES, 2, S // 2], BF16, name="e_sb_%d" % i)
+            e_sb = const.tile([P, Q_TILES, S], BF16, name="e_sb_%d" % i)
             nc.vector.memset(e_sb[:], 0.0)
             e_tiles.append(e_sb)
 
         ident_bf16 = const.tile([P, P], BF16)
         nc.vector.tensor_copy(out=ident_bf16[:], in_=ident_f32[:])
+
+        zeros_f32 = const.tile([P, P], F32)
+        nc.vector.memset(zeros_f32[:], 0.0)
+        low_ps = psum_fixed.tile([P, 2, 2, P], F32)
+        for a in range(2):
+            nc.tensor.transpose(out=low_ps[:, a, 1, :], in_=zeros_f32[:], identity=ident_f32[:])
         bias_of_head = []
         for h in range(H):
             slope = 2.0 ** (-8.0 / H * (h + 1))
@@ -141,11 +152,10 @@ def tile_selfattention_pa_t_kernel(tc, x, Wv, bv, q, k, out):
             xt_ps = psum.tile([P, 2, 2, P], F32, tag="bank")
             for tl in range(2):
                 t = 2 * pair + tl
-                row = 2 * (t % 2) + t // 2
                 for u in range(2):
                     nc.tensor.transpose(
                         out=xt_ps[:, tl, u, :],
-                        in_=x_rows[b][:, row, :].bitcast(F32)[:, P * u : P * (u + 1)],
+                        in_=x_rows[b][:, t, :].bitcast(F32)[:, P * u : P * (u + 1)],
                         identity=ident_f32[:],
                     )
             nc.vector.tensor_copy(
@@ -220,46 +230,47 @@ def tile_selfattention_pa_t_kernel(tc, x, Wv, bv, q, k, out):
             if not live(n):
                 return
             kt_ps = psum.tile([P, 2, 2, P], F32, tag="bank")
-            for u in range(2):
-                for half in range(2):
+            for half in range(2):
+                for u in range(2):
                     nc.tensor.transpose(
-                        out=kt_ps[:, u, half, :],
+                        out=kt_ps[:, half, u, :],
                         in_=k_rows[n][:, half, u, :].bitcast(F32),
                         identity=ident_f32[:],
                     )
             k_t = work.tile([P, 2 * S], BF16, bufs=3)
-            nc.scalar.copy(out=k_t[:].bitcast(F32), in_=kt_ps[:].rearrange("w u a r -> w (u a r)"))
+            nc.scalar.copy(
+                out=k_t[:].bitcast(F32).rearrange("w (half r u) -> w half r u", half=2, u=2),
+                in_=kt_ps[:].rearrange("w half u r -> w half r u"),
+            )
             k_t_of[n] = k_t
 
         def score_tile(n, it):
             if not live(n):
                 return
             q_view = q_t_of[n][:].rearrange("w (a i e) -> w a i e", a=Q_TILES, e=2)
-            k_view = k_t_of[n][:].rearrange("w (u c e) -> w u c e", u=2, e=2)
-            bias_view = bias_of_head[n % H][:].rearrange("i (u c) -> i u c", u=2)
-            width = (P // 2) * (it + 1)
+            k_view = k_t_of[n][:].rearrange("w (j e) -> w j e", e=2)
+            width = P * (it + 1)
             s_ps = psum.tile([P, S], F32, tag="bank")
-            s_view = s_ps[:, : 2 * width].rearrange("i (u c) -> i u c", u=2)
             for e in range(2):
                 nc.tensor.matmul(
-                    out=s_view,
+                    out=s_ps[:, :width],
                     lhsT=q_view[:, it, :, e],
-                    rhs=k_view[:, :, :width, e],
+                    rhs=k_view[:, :width, e],
                     start=(e == 0),
                     stop=False,
                 )
             nc.tensor.matmul(
-                out=s_view,
+                out=s_ps[:, :width],
                 lhsT=ident_bf16[:],
-                rhs=bias_view[:, :, S // 2 - width :],
+                rhs=bias_of_head[n % H][:, S - width :],
                 start=False,
                 stop=True,
             )
             neg_s = small.tile([P, S], F32)
             neg_max = small.tile([P, 1], F32)
             nc.vector.tensor_scalar(
-                out=neg_s[:, : 2 * width],
-                in0=s_ps[:, : 2 * width],
+                out=neg_s[:, :width],
+                in0=s_ps[:, :width],
                 scalar1=-SCORE_SCALE,
                 scalar2=None,
                 op0=ALU.mult,
@@ -275,10 +286,10 @@ def tile_selfattention_pa_t_kernel(tc, x, Wv, bv, q, k, out):
             if n not in sums:
                 row_sum = small.tile([P, Q_TILES], F32)
                 sums[n] = row_sum
-            width = (P // 2) * (it + 1)
+            width = P * (it + 1)
             nc.scalar.activation(
-                out=e_tiles[n % E_COPIES][:, it, :, :width],
-                in_=s_of[(n, it)][:, : 2 * width].rearrange("i (u c) -> i u c", u=2),
+                out=e_tiles[n % E_COPIES][:, it, :width],
+                in_=s_of[(n, it)][:, :width],
                 func=ACT.Exp,
                 bias=neg_max_of[(n, it)][:],
                 scale=-1.0,
@@ -290,12 +301,15 @@ def tile_selfattention_pa_t_kernel(tc, x, Wv, bv, q, k, out):
                 return
             e_grouped = work.tile([P, 2 * S], BF16, align_bytes=64, bufs=4)
             e_grouped_of[(n, pair)] = e_grouped
-            et_ps = psum.tile([P, 2, 2, P], F32, tag="bank")
+            if pair == 0:
+                et_ps = low_ps
+            else:
+                et_ps = psum.tile([P, 2, 2, P], F32, tag="bank")
             for a in range(2):
-                for u in range(2):
+                for u in range(pair + 1):
                     nc.tensor.transpose(
                         out=et_ps[:, a, u, :],
-                        in_=e_tiles[n % E_COPIES][:, 2 * pair + a, u, :].bitcast(F32),
+                        in_=e_tiles[n % E_COPIES][:, 2 * pair + a, :].bitcast(F32)[:, P * u : P * (u + 1)],
                         identity=ident_f32[:],
                     )
             nc.scalar.copy(

@@ -38,6 +38,10 @@ def tile_selfattention_pa_t_kernel(tc, x, Wv, bv, q, k, out):
         psum_fixed = ctx.enter_context(tc.psum_pool(name="psum_fixed", bufs=1))
         ctx.enter_context(tc.manual_schedule())
 
+        zero = const.tile([P, 1], F32)
+        nc.vector.memset(zero[:], 0.0)
+        zeros_f32 = const.tile([P, P], F32)
+        nc.vector.memset(zeros_f32[:], 0.0)
         bv_row = const.tile([P, D], BF16)
         nc.vector.memset(bv_row[:], 0.0)
         ones = const.tile([P, P], BF16)
@@ -91,22 +95,19 @@ def tile_selfattention_pa_t_kernel(tc, x, Wv, bv, q, k, out):
             channel_multiplier=1,
         )
 
-        zero = const.tile([P, 1], F32)
-        nc.vector.memset(zero[:], 0.0)
         one = const.tile([P, 1], F32)
         nc.scalar.activation(out=one[:], in_=zero[:], func=ACT.Exp)
 
         e_tiles = []
         for i in range(E_COPIES):
             e_sb = const.tile([P, Q_TILES, S], BF16, name="e_sb_%d" % i)
-            nc.vector.memset(e_sb[:], 0.0)
+            nc.vector.memset(e_sb[:, 0, P : 2 * P], 0.0)
+            nc.vector.memset(e_sb[:, 2, 3 * P :], 0.0)
             e_tiles.append(e_sb)
 
         ident_bf16 = const.tile([P, P], BF16)
         nc.vector.tensor_copy(out=ident_bf16[:], in_=ident_f32[:])
 
-        zeros_f32 = const.tile([P, P], F32)
-        nc.vector.memset(zeros_f32[:], 0.0)
         low_ps = psum_fixed.tile([P, 2, 2, P], F32)
         for a in range(2):
             nc.tensor.transpose(out=low_ps[:, a, 1, :], in_=zeros_f32[:], identity=ident_f32[:])

@@ -46,6 +46,15 @@ def tile_selfattention_pa_t_kernel(tc, x, Wv, bv, q, k, out):
         nc.vector.memset(bv_row[:], 0.0)
         ones = const.tile([P, P], BF16)
         nc.vector.memset(ones[:], 1.0)
+        idle_rhs = const.tile([P, S], BF16)
+        nc.vector.memset(idle_rhs[:], 0.0)
+
+        def keep_warm(count):
+            idle_ps = psum.tile([P, S], F32, tag="bank")
+            for i in range(count):
+                nc.tensor.matmul(out=idle_ps[:], lhsT=ones[:], rhs=idle_rhs[:], start=True, stop=True)
+
+        keep_warm(4)
 
         wv_raw = const.tile([P, PACK, D], BF16)
         x_rows, q_rows, k_rows = [], [], []
@@ -372,8 +381,12 @@ def tile_selfattention_pa_t_kernel(tc, x, Wv, bv, q, k, out):
             transpose_e(n - 1, 0)
             exponential(n, 2)
             transpose_q(n + 2)
+            if n == -1:
+                keep_warm(1)
             exponential(n, 1)
             transpose_k(n + 2)
+            if n == -2:
+                keep_warm(4)
             exponential(n, 0)
             quantise_v(n - 1)
             transpose_x(n + 2)

@@ -11,6 +11,7 @@ U8 = mybir.dt.uint8
 FP8X4 = mybir.dt.float8_e4m3fn_x4
 ALU = mybir.AluOpType
 ACT = mybir.ActivationFunctionType
+AXIS = mybir.AxisListType
 
 B, S, D, H = 8, 512, 512, 2
 HD = D // H
@@ -22,6 +23,7 @@ SCORE_SCALE = 1.0 / math.sqrt(HD)
 MASKED = -3.0e38
 E_COPIES = 3
 PSUM_BANKS = 8
+VECTOR_BIAS_TILES = 1
 ROTATING_BANKS = PSUM_BANKS - 1
 
 FLOPS = 2 * B * S * D * D + 2 * (2 * B * H * S * S * HD)
@@ -126,6 +128,14 @@ def tile_selfattention_pa_t_kernel(tc, x, Wv, bv, q, k, out):
             bias_bf16 = const.tile([P, S], BF16, name="bias_bf16_%d" % h)
             nc.vector.tensor_scalar_mul(out=bias_bf16[:], in0=bias_f32[:], scalar1=slope / SCORE_SCALE)
             bias_of_head.append(bias_bf16)
+        neg_bias_of_head = []
+        for h in range(H):
+            slope = 2.0 ** (-8.0 / H * (h + 1))
+            neg_bias = const.tile([P, VECTOR_BIAS_TILES * P], F32, name="neg_bias_%d" % h)
+            nc.vector.tensor_scalar_mul(
+                out=neg_bias[:], in0=bias_f32[:, S - VECTOR_BIAS_TILES * P :], scalar1=-slope
+            )
+            neg_bias_of_head.append(neg_bias)
 
         wv_grouped = const.tile([P, D, PACK], BF16, align_bytes=64)
         nc.vector.tensor_copy(out=wv_grouped[:], in_=wv_raw[:].rearrange("w t n -> w n t"))
@@ -261,34 +271,52 @@ def tile_selfattention_pa_t_kernel(tc, x, Wv, bv, q, k, out):
             k_view = k_t_of[n][:].rearrange("w (j e) -> w j e", e=2)
             width = P * (it + 1)
             s_ps = psum.tile([P, S], F32, tag="bank")
+            on_vector = it < VECTOR_BIAS_TILES
             for e in range(2):
                 nc.tensor.matmul(
                     out=s_ps[:, :width],
                     lhsT=q_view[:, it, :, e],
                     rhs=k_view[:, :width, e],
                     start=(e == 0),
-                    stop=False,
+                    stop=(on_vector and e == 1),
                 )
-            nc.tensor.matmul(
-                out=s_ps[:, :width],
-                lhsT=ident_bf16[:],
-                rhs=bias_of_head[n % H][:, S - width :],
-                start=False,
-                stop=True,
-            )
             neg_s = small.tile([P, S], F32)
             neg_max = small.tile([P, 1], F32)
-            nc.vector.tensor_scalar(
-                out=neg_s[:, :width],
-                in0=s_ps[:, :width],
-                scalar1=-SCORE_SCALE,
-                scalar2=None,
-                op0=ALU.mult,
-                op1=ALU.min,
-                accum_out=neg_max[:],
-            )
+            if on_vector:
+                nc.vector.scalar_tensor_tensor(
+                    out=neg_s[:, :width],
+                    in0=s_ps[:, :width],
+                    scalar=-SCORE_SCALE,
+                    in1=neg_bias_of_head[n % H][:, VECTOR_BIAS_TILES * P - width :],
+                    op0=ALU.mult,
+                    op1=ALU.add,
+                )
+            else:
+                nc.tensor.matmul(
+                    out=s_ps[:, :width],
+                    lhsT=ident_bf16[:],
+                    rhs=bias_of_head[n % H][:, S - width :],
+                    start=False,
+                    stop=True,
+                )
+                nc.vector.tensor_scalar(
+                    out=neg_s[:, :width],
+                    in0=s_ps[:, :width],
+                    scalar1=-SCORE_SCALE,
+                    scalar2=None,
+                    op0=ALU.mult,
+                    op1=ALU.min,
+                    accum_out=neg_max[:],
+                )
             s_of[(n, it)] = neg_s
             neg_max_of[(n, it)] = neg_max
+
+        def row_minimum(n, it):
+            if not live(n) or it >= VECTOR_BIAS_TILES:
+                return
+            nc.vector.tensor_reduce(
+                out=neg_max_of[(n, it)][:], in_=s_of[(n, it)][:, : P * (it + 1)], op=ALU.min, axis=AXIS.X
+            )
 
         def exponential(n, it):
             if not live(n):
@@ -387,9 +415,10 @@ def tile_selfattention_pa_t_kernel(tc, x, Wv, bv, q, k, out):
             transpose_k(n + 2)
             if n == -2:
                 keep_warm(4)
-            exponential(n, 0)
             quantise_v(n - 1)
             transpose_x(n + 2)
+            row_minimum(n, 0)
+            exponential(n, 0)
             quantise_x(n + 2)
             context(n - 3, 1)
             project_v(n, 0)

@@ -24,7 +24,6 @@ MASKED = -3.0e38
 E_COPIES = 3
 PSUM_BANKS = 8
 VECTOR_BIAS_TILES = 1
-ROTATING_BANKS = PSUM_BANKS - 1
 
 FLOPS = 2 * B * S * D * D + 2 * (2 * B * H * S * S * HD)
 
@@ -36,14 +35,11 @@ def tile_selfattention_pa_t_kernel(tc, x, Wv, bv, q, k, out):
         loads = ctx.enter_context(tc.tile_pool(name="loads", bufs=HEADS))
         work = ctx.enter_context(tc.tile_pool(name="work", bufs=2))
         small = ctx.enter_context(tc.tile_pool(name="small", bufs=8))
-        psum = ctx.enter_context(tc.psum_pool(name="psum", bufs=ROTATING_BANKS))
-        psum_fixed = ctx.enter_context(tc.psum_pool(name="psum_fixed", bufs=1))
+        psum = ctx.enter_context(tc.psum_pool(name="psum", bufs=PSUM_BANKS))
         ctx.enter_context(tc.manual_schedule())
 
         zero = const.tile([P, 1], F32)
         nc.vector.memset(zero[:], 0.0)
-        zeros_f32 = const.tile([P, P], F32)
-        nc.vector.memset(zeros_f32[:], 0.0)
         bv_row = const.tile([P, D], BF16)
         nc.vector.memset(bv_row[:], 0.0)
         ones = const.tile([P, P], BF16)
@@ -119,9 +115,11 @@ def tile_selfattention_pa_t_kernel(tc, x, Wv, bv, q, k, out):
         ident_bf16 = const.tile([P, P], BF16)
         nc.vector.tensor_copy(out=ident_bf16[:], in_=ident_f32[:])
 
-        low_ps = psum_fixed.tile([P, 2, 2, P], F32)
-        for a in range(2):
-            nc.tensor.transpose(out=low_ps[:, a, 1, :], in_=zeros_f32[:], identity=ident_f32[:])
+        e_grouped_tiles = []
+        for i in range(E_COPIES):
+            e_grouped = const.tile([P, Q_TILES, P, PACK], BF16, align_bytes=64, name="e_grouped_%d" % i)
+            nc.gpsimd.memset(e_grouped[:, :2].rearrange("p a i t -> p (a i t)").bitcast(F32), 0.0)
+            e_grouped_tiles.append(e_grouped)
         bias_of_head = []
         for h in range(H):
             slope = 2.0 ** (-8.0 / H * (h + 1))
@@ -149,7 +147,7 @@ def tile_selfattention_pa_t_kernel(tc, x, Wv, bv, q, k, out):
 
         x_grouped_of, x_mx, v_grouped_of, v_mx = {}, {}, {}, {}
         q_t_of, k_t_of, s_of, neg_max_of, sums = {}, {}, {}, {}, {}
-        e_grouped_of, e_mx, inv_of = {}, {}, {}
+        e_mx, inv_of = {}, {}
 
         def live(n):
             return 0 <= n < HEADS
@@ -321,9 +319,10 @@ def tile_selfattention_pa_t_kernel(tc, x, Wv, bv, q, k, out):
         def exponential(n, it):
             if not live(n):
                 return
-            if n not in sums:
-                row_sum = small.tile([P, Q_TILES], F32)
-                sums[n] = row_sum
+            b, h = n // H, n % H
+            if b not in sums:
+                row_sum = small.tile([P, H, Q_TILES], F32)
+                sums[b] = row_sum
             width = P * (it + 1)
             nc.scalar.activation(
                 out=e_tiles[n % E_COPIES][:, it, :width],
@@ -331,54 +330,72 @@ def tile_selfattention_pa_t_kernel(tc, x, Wv, bv, q, k, out):
                 func=ACT.Exp,
                 bias=neg_max_of[(n, it)][:],
                 scale=-1.0,
-                accum_out=sums[n][:, it : it + 1],
+                accum_out=sums[b][:, h, it : it + 1],
             )
 
         def transpose_e(n, pair):
             if not live(n):
                 return
-            e_grouped = work.tile([P, 2 * S], BF16, align_bytes=64, bufs=4)
-            e_grouped_of[(n, pair)] = e_grouped
-            if pair == 0:
-                et_ps = low_ps
-            else:
-                et_ps = psum.tile([P, 2, 2, P], F32, tag="bank")
+            units = pair + 1
+            et_ps = psum.tile([P, 2, units, P], F32, tag="bank")
             for a in range(2):
-                for u in range(pair + 1):
+                for u in range(units):
                     nc.tensor.transpose(
                         out=et_ps[:, a, u, :],
                         in_=e_tiles[n % E_COPIES][:, 2 * pair + a, :].bitcast(F32)[:, P * u : P * (u + 1)],
                         identity=ident_f32[:],
                     )
+            grouped = e_grouped_tiles[n % E_COPIES]
+            if pair == 1:
+                nc.scalar.copy(
+                    out=grouped[:, 2:].rearrange("p a i t -> p (a i t)").bitcast(F32).rearrange(
+                        "p (a i u) -> p a i u", a=2, u=2
+                    ),
+                    in_=et_ps[:].rearrange("p a u i -> p a i u"),
+                )
+                return
+            e_low = work.tile([P, 2, 2 * P], BF16)
             nc.scalar.copy(
-                out=e_grouped[:].bitcast(F32).rearrange("p (a i u) -> p a i u", a=2, u=2),
-                in_=et_ps[:].rearrange("p a u i -> p a i u"),
+                out=e_low[:].rearrange("p a m -> p (a m)").bitcast(F32),
+                in_=et_ps[:].rearrange("p a u i -> p (a u i)"),
             )
+            for a in range(2):
+                nc.gpsimd.tensor_scalar(
+                    out=grouped[:, a, :, 0:2],
+                    in0=e_low[:, a, :].rearrange("p (i o) -> p i o", o=2),
+                    scalar1=1.0,
+                    scalar2=0.0,
+                    op0=ALU.mult,
+                    op1=ALU.add,
+                )
 
-        def quantise_e(n, pair):
+        def quantise_e(n):
             if not live(n):
                 return
-            e_codes = work.tile([P, S // 2], U32, align_bytes=64, bufs=4)
-            e_scales = work.tile([P, S // 2], U8, align_bytes=64, bufs=4)
+            e_codes = work.tile([P, S], U32, align_bytes=64)
+            e_scales = work.tile([P, S], U8, align_bytes=64)
             nc.vector.quantize_mx(
-                out=e_codes[:].bitcast(FP8X4), scales=e_scales[:], in_=e_grouped_of[(n, pair)][:]
+                out=e_codes[:].bitcast(FP8X4),
+                scales=e_scales[:],
+                in_=e_grouped_tiles[n % E_COPIES][:].rearrange("p it i t -> p (it i t)"),
             )
-            e_mx[(n, pair)] = (e_codes, e_scales)
+            e_mx[n] = (e_codes, e_scales)
 
         def context(n, pair):
             if not live(n):
                 return
             b, h = n // H, n % H
-            e_codes, e_scales = e_mx[(n, pair)]
+            e_codes, e_scales = e_mx[n]
             v_codes, v_scales = v_mx[b]
             dims = slice(HD * h, HD * (h + 1))
-            if n not in inv_of:
-                inv_sum = small.tile([P, Q_TILES], F32)
-                nc.vector.reciprocal(out=inv_sum[:], in_=sums[n][:])
-                inv_of[n] = inv_sum
+            if b not in inv_of:
+                inv_sum = small.tile([P, H, Q_TILES], F32)
+                nc.vector.reciprocal(out=inv_sum[:], in_=sums[b][:])
+                inv_of[b] = inv_sum
             c_ps = psum.tile([P, 2, HD], F32, tag="bank")
             for a in range(2):
-                queries = slice(P * a, P * (a + 1))
+                it = 2 * pair + a
+                queries = slice(P * it, P * (it + 1))
                 nc.tensor.matmul_mx(
                     out=c_ps[:, a, :],
                     lhsT=e_codes[:, queries].bitcast(FP8X4),
@@ -392,7 +409,7 @@ def tile_selfattention_pa_t_kernel(tc, x, Wv, bv, q, k, out):
             for a in range(2):
                 it = 2 * pair + a
                 nc.scalar.activation(
-                    out=ctx_sb[:, a, :], in_=c_ps[:, a, :], func=ACT.Copy, scale=inv_of[n][:, it : it + 1]
+                    out=ctx_sb[:, a, :], in_=c_ps[:, a, :], func=ACT.Copy, scale=inv_of[b][:, h, it : it + 1]
                 )
             rows = slice(2 * P * pair, 2 * P * (pair + 1))
             nc.sync.dma_start(out=out[b, rows, dims].rearrange("(a p) d -> p a d", p=P), in_=ctx_sb[:])
@@ -402,8 +419,7 @@ def tile_selfattention_pa_t_kernel(tc, x, Wv, bv, q, k, out):
             score_tile(n, 2)
             transpose_e(n - 1, 1)
             exponential(n, 3)
-            quantise_e(n - 2, 1)
-            quantise_e(n - 2, 0)
+            quantise_e(n - 2)
             score_tile(n, 1)
             score_tile(n, 0)
             transpose_e(n - 1, 0)

@@ -419,7 +419,8 @@ def tile_selfattention_pa_t_kernel(tc, x, Wv, bv, q, k, out):
             score_tile(n, 2)
             transpose_e(n - 1, 1)
             exponential(n, 3)
-            quantise_e(n - 2)
+            quantise_x(n + 1)
+            quantise_v(n - 2)
             score_tile(n, 1)
             score_tile(n, 0)
             transpose_e(n - 1, 0)
@@ -431,13 +432,12 @@ def tile_selfattention_pa_t_kernel(tc, x, Wv, bv, q, k, out):
             transpose_k(n + 2)
             if n == -2:
                 keep_warm(4)
-            quantise_v(n - 1)
             transpose_x(n + 2)
             row_minimum(n, 0)
             exponential(n, 0)
-            quantise_x(n + 2)
             context(n - 3, 1)
             project_v(n, 0)
+            quantise_e(n - 2)
             context(n - 3, 0)
             project_v(n, 1)
             if n == -2:

@@ -422,7 +422,6 @@ def tile_selfattention_pa_t_kernel(tc, x, Wv, bv, q, k, out):
             quantise_x(n + 1)
             quantise_v(n - 2)
             score_tile(n, 1)
-            score_tile(n, 0)
             transpose_e(n - 1, 0)
             exponential(n, 2)
             transpose_q(n + 2)
@@ -433,10 +432,11 @@ def tile_selfattention_pa_t_kernel(tc, x, Wv, bv, q, k, out):
             if n == -2:
                 keep_warm(4)
             transpose_x(n + 2)
+            score_tile(n, 0)
+            project_v(n, 0)
+            context(n - 3, 1)
             row_minimum(n, 0)
             exponential(n, 0)
-            context(n - 3, 1)
-            project_v(n, 0)
             quantise_e(n - 2)
             context(n - 3, 0)
             project_v(n, 1)

@@ -59,26 +59,34 @@ def tile_selfattention_pa_t_kernel(tc, x, Wv, bv, q, k, out):
         for n in range(HEADS):
             b, h = n // H, n % H
             q_sb = loads.tile([P, Q_TILES, HD], BF16)
-            nc.sync.dma_start(out=q_sb[:], in_=q[b, h].rearrange("(it p) d -> p it d", p=P))
             q_rows.append(q_sb)
             k_sb = loads.tile([P, 2, 2, HD], BF16)
-            nc.sync.dma_start(
-                out=k_sb[:], in_=k[b, h].rearrange("(half r u) d -> r half u d", half=2, u=2)
-            )
             k_rows.append(k_sb)
+            q_view = q[b, h].rearrange("(it p) d -> p it d", p=P)
+            k_view = k[b, h].rearrange("(half r u) d -> r half u d", half=2, u=2)
             if n == 0:
+                for half in range(2):
+                    tiles = slice(2 * half, 2 * half + 2)
+                    nc.sync.dma_start(out=q_sb[:, tiles], in_=q_view[:, tiles])
+                    nc.sync.dma_start(out=k_sb[:, half : half + 1], in_=k_view[:, half : half + 1])
+            else:
+                nc.sync.dma_start(out=q_sb[:], in_=q_view)
+                nc.sync.dma_start(out=k_sb[:], in_=k_view)
+            if n == 0:
+                continue
+            if n == 1:
                 nc.sync.dma_start(
                     out=wv_raw[:].rearrange("w (u e) n -> w u e n", u=2),
                     in_=Wv.rearrange("(u w e) n -> w u e n", u=2, e=2),
                 )
-            if h == 0:
+            if n == 1 or h == 0:
                 x_sb = loads.tile([P, PACK, D], BF16, bufs=B)
                 nc.sync.dma_start(
                     out=x_sb[:].rearrange("p (u e) f -> p u e f", u=2),
                     in_=x[b].rearrange("(u p e) f -> p u e f", u=2, e=2),
                 )
                 x_rows.append(x_sb)
-            if n == 0:
+            if n == 1:
                 nc.sync.dma_start(out=bv_row[0:1, :], in_=bv.rearrange("(o n) -> o n", o=1))
 
         ident_f32 = const.tile([P, P], F32)
@@ -118,7 +126,6 @@ def tile_selfattention_pa_t_kernel(tc, x, Wv, bv, q, k, out):
         e_grouped_tiles = []
         for i in range(E_COPIES):
             e_grouped = const.tile([P, Q_TILES, P, PACK], BF16, align_bytes=64, name="e_grouped_%d" % i)
-            nc.gpsimd.memset(e_grouped[:, :2].rearrange("p a i t -> p (a i t)").bitcast(F32), 0.0)
             e_grouped_tiles.append(e_grouped)
         bias_of_head = []
         for h in range(H):
@@ -136,14 +143,27 @@ def tile_selfattention_pa_t_kernel(tc, x, Wv, bv, q, k, out):
             neg_bias_of_head.append(neg_bias)
 
         wv_grouped = const.tile([P, D, PACK], BF16, align_bytes=64)
-        nc.vector.tensor_copy(out=wv_grouped[:], in_=wv_raw[:].rearrange("w t n -> w n t"))
+        for c in range(H):
+            cols = slice(HD * c, HD * (c + 1))
+            nc.gpsimd.tensor_scalar(
+                out=wv_grouped[:, cols, :],
+                in0=wv_raw[:, :, cols].rearrange("w t n -> w n t"),
+                scalar1=1.0,
+                scalar2=0.0,
+                op0=ALU.mult,
+                op1=ALU.add,
+            )
+        for e_grouped in e_grouped_tiles:
+            nc.gpsimd.memset(e_grouped[:, :2].rearrange("p a i t -> p (a i t)").bitcast(F32), 0.0)
         wv_codes = const.tile([P, D], U32, align_bytes=64)
         wv_scales = const.tile([P, D], U8, align_bytes=64)
-        nc.vector.quantize_mx(
-            out=wv_codes[:].bitcast(FP8X4),
-            scales=wv_scales[:],
-            in_=wv_grouped[:].rearrange("w n t -> w (n t)"),
-        )
+
+        def quantise_wv():
+            nc.vector.quantize_mx(
+                out=wv_codes[:].bitcast(FP8X4),
+                scales=wv_scales[:],
+                in_=wv_grouped[:].rearrange("w n t -> w (n t)"),
+            )
 
         x_grouped_of, x_mx, v_grouped_of, v_mx = {}, {}, {}, {}
         q_t_of, k_t_of, s_of, neg_max_of, sums = {}, {}, {}, {}, {}
@@ -157,7 +177,7 @@ def tile_selfattention_pa_t_kernel(tc, x, Wv, bv, q, k, out):
         def spread_bv():
             bv_ps = psum.tile([P, D], F32, tag="bank")
             nc.tensor.matmul(out=bv_ps[:], lhsT=ones[:], rhs=bv_row[:], start=True, stop=True)
-            nc.vector.tensor_copy(out=bv_all[:], in_=bv_ps[:])
+            nc.scalar.copy(out=bv_all[:], in_=bv_ps[:])
 
         def transpose_x(m):
             if not live(m):
@@ -232,35 +252,43 @@ def tile_selfattention_pa_t_kernel(tc, x, Wv, bv, q, k, out):
             )
             v_mx[b] = (v_codes, v_scales)
 
-        def transpose_q(n):
+        def transpose_q(n, halves=(0, 1)):
             if not live(n):
                 return
-            qt_ps = psum.tile([P, Q_TILES, P], F32, tag="bank")
-            for it in range(Q_TILES):
+            if n not in q_t_of:
+                q_t = work.tile([P, 2 * S], BF16, bufs=3)
+                q_t_of[n] = q_t
+            first, count = 2 * halves[0], 2 * len(halves)
+            qt_ps = psum.tile([P, count, P], F32, tag="bank")
+            for a in range(count):
                 nc.tensor.transpose(
-                    out=qt_ps[:, it, :], in_=q_rows[n][:, it, :].bitcast(F32), identity=ident_f32[:]
+                    out=qt_ps[:, a, :], in_=q_rows[n][:, first + a, :].bitcast(F32), identity=ident_f32[:]
                 )
-            q_t = work.tile([P, 2 * S], BF16, bufs=3)
-            nc.scalar.copy(out=q_t[:].bitcast(F32), in_=qt_ps[:].rearrange("w a i -> w (a i)"))
-            q_t_of[n] = q_t
+            nc.scalar.copy(
+                out=q_t_of[n][:].bitcast(F32)[:, P * first : P * (first + count)],
+                in_=qt_ps[:].rearrange("w a i -> w (a i)"),
+            )
 
-        def transpose_k(n):
+        def transpose_k(n, halves=(0, 1)):
             if not live(n):
                 return
-            kt_ps = psum.tile([P, 2, 2, P], F32, tag="bank")
-            for half in range(2):
+            if n not in k_t_of:
+                k_t = work.tile([P, 2 * S], BF16, bufs=3)
+                k_t_of[n] = k_t
+            count = len(halves)
+            kt_ps = psum.tile([P, count, 2, P], F32, tag="bank")
+            for a in range(count):
                 for u in range(2):
                     nc.tensor.transpose(
-                        out=kt_ps[:, half, u, :],
-                        in_=k_rows[n][:, half, u, :].bitcast(F32),
+                        out=kt_ps[:, a, u, :],
+                        in_=k_rows[n][:, halves[a], u, :].bitcast(F32),
                         identity=ident_f32[:],
                     )
-            k_t = work.tile([P, 2 * S], BF16, bufs=3)
+            keys = slice(2 * P * halves[0], 2 * P * (halves[0] + count))
             nc.scalar.copy(
-                out=k_t[:].bitcast(F32).rearrange("w (half r u) -> w half r u", half=2, u=2),
+                out=k_t_of[n][:].bitcast(F32)[:, keys].rearrange("w (half r u) -> w half r u", half=count, u=2),
                 in_=kt_ps[:].rearrange("w half u r -> w half r u"),
             )
-            k_t_of[n] = k_t
 
         def score_tile(n, it):
             if not live(n):
@@ -333,7 +361,7 @@ def tile_selfattention_pa_t_kernel(tc, x, Wv, bv, q, k, out):
                 accum_out=sums[b][:, h, it : it + 1],
             )
 
-        def transpose_e(n, pair):
+        def transpose_e(n, pair, by_scalar=False):
             if not live(n):
                 return
             units = pair + 1
@@ -354,6 +382,11 @@ def tile_selfattention_pa_t_kernel(tc, x, Wv, bv, q, k, out):
                     in_=et_ps[:].rearrange("p a u i -> p a i u"),
                 )
                 return
+            if by_scalar:
+                for a in range(2):
+                    words = grouped[:, a].rearrange("p i t -> p (i t)").bitcast(F32)
+                    nc.scalar.copy(out=words.rearrange("p (i u) -> p i u", u=2)[:, :, 0], in_=et_ps[:, a, 0, :])
+                return
             e_low = work.tile([P, 2, 2 * P], BF16)
             nc.scalar.copy(
                 out=e_low[:].rearrange("p a m -> p (a m)").bitcast(F32),
@@ -369,19 +402,22 @@ def tile_selfattention_pa_t_kernel(tc, x, Wv, bv, q, k, out):
                     op1=ALU.add,
                 )
 
-        def quantise_e(n):
+        def quantise_e(n, first=0, last=Q_TILES):
             if not live(n):
                 return
-            e_codes = work.tile([P, S], U32, align_bytes=64)
-            e_scales = work.tile([P, S], U8, align_bytes=64)
+            if n not in e_mx:
+                e_codes = work.tile([P, S], U32, align_bytes=64)
+                e_scales = work.tile([P, S], U8, align_bytes=64)
+                e_mx[n] = (e_codes, e_scales)
+            e_codes, e_scales = e_mx[n]
+            queries = slice(P * first, P * last)
             nc.vector.quantize_mx(
-                out=e_codes[:].bitcast(FP8X4),
-                scales=e_scales[:],
-                in_=e_grouped_tiles[n % E_COPIES][:].rearrange("p it i t -> p (it i t)"),
+                out=e_codes[:, queries].bitcast(FP8X4),
+                scales=e_scales[:, queries],
+                in_=e_grouped_tiles[n % E_COPIES][:, first:last].rearrange("p it i t -> p (it i t)"),
             )
-            e_mx[n] = (e_codes, e_scales)
 
-        def context(n, pair):
+        def context(n, pair, by_vector=False):
             if not live(n):
                 return
             b, h = n // H, n % H
@@ -408,13 +444,57 @@ def tile_selfattention_pa_t_kernel(tc, x, Wv, bv, q, k, out):
             ctx_sb = work.tile([P, 2, HD], F32, bufs=6)
             for a in range(2):
                 it = 2 * pair + a
-                nc.scalar.activation(
-                    out=ctx_sb[:, a, :], in_=c_ps[:, a, :], func=ACT.Copy, scale=inv_of[b][:, h, it : it + 1]
-                )
+                inv = inv_of[b][:, h, it : it + 1]
+                if by_vector:
+                    nc.vector.tensor_scalar_mul(out=ctx_sb[:, a, :], in0=c_ps[:, a, :], scalar1=inv)
+                else:
+                    nc.scalar.activation(out=ctx_sb[:, a, :], in_=c_ps[:, a, :], func=ACT.Copy, scale=inv)
             rows = slice(2 * P * pair, 2 * P * (pair + 1))
             nc.sync.dma_start(out=out[b, rows, dims].rearrange("(a p) d -> p a d", p=P), in_=ctx_sb[:])
 
-        for n in range(-2, HEADS + 3):
+        transpose_q(0, (0,))
+        transpose_k(0, (0,))
+        transpose_q(0, (1,))
+        transpose_k(0, (1,))
+        score_tile(0, 1)
+        score_tile(0, 0)
+        score_tile(0, 3)
+        score_tile(0, 2)
+        exponential(0, 1)
+        transpose_q(1)
+        row_minimum(0, 0)
+        transpose_k(1)
+        exponential(0, 0)
+        transpose_x(0)
+        exponential(0, 3)
+        score_tile(1, 3)
+        score_tile(1, 2)
+        exponential(0, 2)
+        transpose_x(1)
+        spread_bv()
+        exponential(1, 3)
+        quantise_wv()
+        transpose_e(0, 1)
+        score_tile(1, 1)
+        quantise_x(1)
+        transpose_e(0, 0)
+        exponential(1, 2)
+        transpose_q(2)
+        exponential(1, 1)
+        transpose_k(2)
+        score_tile(1, 0)
+        transpose_x(2)
+        project_v(0, 0)
+        project_v(0, 1)
+        row_minimum(1, 0)
+        exponential(1, 0)
+        project_v(1, 0)
+        transpose_q(3)
+        transpose_k(3)
+        transpose_x(3)
+        project_v(1, 1)
+
+        for n in range(2, HEADS):
             score_tile(n, 3)
             score_tile(n, 2)
             transpose_e(n - 1, 1)
@@ -425,12 +505,8 @@ def tile_selfattention_pa_t_kernel(tc, x, Wv, bv, q, k, out):
             transpose_e(n - 1, 0)
             exponential(n, 2)
             transpose_q(n + 2)
-            if n == -1:
-                keep_warm(1)
             exponential(n, 1)
             transpose_k(n + 2)
-            if n == -2:
-                keep_warm(4)
             transpose_x(n + 2)
             score_tile(n, 0)
             project_v(n, 0)
@@ -440,5 +516,17 @@ def tile_selfattention_pa_t_kernel(tc, x, Wv, bv, q, k, out):
             quantise_e(n - 2)
             context(n - 3, 0)
             project_v(n, 1)
-            if n == -2:
-                spread_bv()
+
+        last = HEADS - 1
+        transpose_e(last, 1)
+        quantise_v(last)
+        context(last - 2, 1)
+        quantise_e(last - 1)
+        transpose_e(last, 0, by_scalar=True)
+        context(last - 2, 0, by_vector=True)
+        context(last - 1, 1)
+        quantise_e(last, 2, 4)
+        context(last - 1, 0, by_vector=True)
+        quantise_e(last, 0, 2)
+        context(last, 1)
+        context(last, 0, by_vector=True)

@@ -74,11 +74,6 @@ def tile_selfattention_pa_t_kernel(tc, x, Wv, bv, q, k, out):
                 nc.sync.dma_start(out=k_sb[:], in_=k_view)
             if n == 0:
                 continue
-            if n == 1:
-                nc.sync.dma_start(
-                    out=wv_raw[:].rearrange("w (u e) n -> w u e n", u=2),
-                    in_=Wv.rearrange("(u w e) n -> w u e n", u=2, e=2),
-                )
             if n == 1 or h == 0:
                 x_sb = loads.tile([P, PACK, D], BF16, bufs=B)
                 nc.sync.dma_start(
@@ -88,6 +83,10 @@ def tile_selfattention_pa_t_kernel(tc, x, Wv, bv, q, k, out):
                 x_rows.append(x_sb)
             if n == 1:
                 nc.sync.dma_start(out=bv_row[0:1, :], in_=bv.rearrange("(o n) -> o n", o=1))
+                nc.sync.dma_start(
+                    out=wv_raw[:].rearrange("w (u e) n -> w u e n", u=2),
+                    in_=Wv.rearrange("(u w e) n -> w u e n", u=2, e=2),
+                )
 
         ident_f32 = const.tile([P, P], F32)
         make_identity(nc, ident_f32[:])
@@ -126,6 +125,7 @@ def tile_selfattention_pa_t_kernel(tc, x, Wv, bv, q, k, out):
         e_grouped_tiles = []
         for i in range(E_COPIES):
             e_grouped = const.tile([P, Q_TILES, P, PACK], BF16, align_bytes=64, name="e_grouped_%d" % i)
+            nc.gpsimd.memset(e_grouped[:, :2].rearrange("p a i t -> p (a i t)").bitcast(F32), 0.0)
             e_grouped_tiles.append(e_grouped)
         bias_of_head = []
         for h in range(H):
@@ -153,8 +153,6 @@ def tile_selfattention_pa_t_kernel(tc, x, Wv, bv, q, k, out):
                 op0=ALU.mult,
                 op1=ALU.add,
             )
-        for e_grouped in e_grouped_tiles:
-            nc.gpsimd.memset(e_grouped[:, :2].rearrange("p a i t -> p (a i t)").bitcast(F32), 0.0)
         wv_codes = const.tile([P, D], U32, align_bytes=64)
         wv_scales = const.tile([P, D], U8, align_bytes=64)
 
@@ -459,24 +457,24 @@ def tile_selfattention_pa_t_kernel(tc, x, Wv, bv, q, k, out):
         score_tile(0, 1)
         score_tile(0, 0)
         score_tile(0, 3)
-        score_tile(0, 2)
         exponential(0, 1)
         transpose_q(1)
         row_minimum(0, 0)
         transpose_k(1)
+        score_tile(0, 2)
         exponential(0, 0)
         transpose_x(0)
+        transpose_x(1)
         exponential(0, 3)
+        spread_bv()
         score_tile(1, 3)
         score_tile(1, 2)
         exponential(0, 2)
-        transpose_x(1)
-        spread_bv()
         exponential(1, 3)
+        quantise_x(1)
         quantise_wv()
         transpose_e(0, 1)
         score_tile(1, 1)
-        quantise_x(1)
         transpose_e(0, 0)
         exponential(1, 2)
         transpose_q(2)

@@ -295,7 +295,7 @@ def tile_selfattention_pa_t_kernel(tc, x, Wv, bv, q, k, out):
             k_view = k_t_of[n][:].rearrange("w (j e) -> w j e", e=2)
             width = P * (it + 1)
             s_ps = psum.tile([P, S], F32, tag="bank")
-            on_vector = it < VECTOR_BIAS_TILES
+            on_vector = it < VECTOR_BIAS_TILES and n % H == 0
             for e in range(2):
                 nc.tensor.matmul(
                     out=s_ps[:, :width],
@@ -336,7 +336,7 @@ def tile_selfattention_pa_t_kernel(tc, x, Wv, bv, q, k, out):
             neg_max_of[(n, it)] = neg_max
 
         def row_minimum(n, it):
-            if not live(n) or it >= VECTOR_BIAS_TILES:
+            if not live(n) or it >= VECTOR_BIAS_TILES or n % H:
                 return
             nc.vector.tensor_reduce(
                 out=neg_max_of[(n, it)][:], in_=s_of[(n, it)][:, : P * (it + 1)], op=ALU.min, axis=AXIS.X

@@ -58,20 +58,19 @@ def tile_selfattention_pa_t_kernel(tc, x, Wv, bv, q, k, out):
         x_rows, q_rows, k_rows = [], [], []
         for n in range(HEADS):
             b, h = n // H, n % H
+            halves = 2 if n == 0 else 1
+            in_row = Q_TILES // halves
             q_sb = loads.tile([P, Q_TILES, HD], BF16)
             q_rows.append(q_sb)
-            k_sb = loads.tile([P, 2, 2, HD], BF16)
+            k_sb = loads.tile([P, Q_TILES, HD], BF16)
             k_rows.append(k_sb)
-            q_view = q[b, h].rearrange("(it p) d -> p it d", p=P)
-            k_view = k[b, h].rearrange("(half r u) d -> r half u d", half=2, u=2)
-            if n == 0:
-                for half in range(2):
-                    tiles = slice(2 * half, 2 * half + 2)
-                    nc.sync.dma_start(out=q_sb[:, tiles], in_=q_view[:, tiles])
-                    nc.sync.dma_start(out=k_sb[:, half : half + 1], in_=k_view[:, half : half + 1])
-            else:
-                nc.sync.dma_start(out=q_sb[:], in_=q_view)
-                nc.sync.dma_start(out=k_sb[:], in_=k_view)
+            for half in range(halves):
+                rows = slice(S // halves * half, S // halves * (half + 1))
+                slots = slice(in_row * half, in_row * (half + 1))
+                for dst, src in ((q_sb, q), (k_sb, k)):
+                    nc.sync.dma_start(
+                        out=dst[:, slots], in_=src[b, h, rows].rearrange("(p u) d -> p u d", u=in_row)
+                    )
             if n == 0:
                 continue
             if n == 1 or h == 0:
@@ -125,8 +124,12 @@ def tile_selfattention_pa_t_kernel(tc, x, Wv, bv, q, k, out):
         e_grouped_tiles = []
         for i in range(E_COPIES):
             e_grouped = const.tile([P, Q_TILES, P, PACK], BF16, align_bytes=64, name="e_grouped_%d" % i)
-            nc.gpsimd.memset(e_grouped[:, :2].rearrange("p a i t -> p (a i t)").bitcast(F32), 0.0)
             e_grouped_tiles.append(e_grouped)
+
+        def zero_low_tiles(i):
+            nc.gpsimd.memset(e_grouped_tiles[i][:, :2].rearrange("p a i t -> p (a i t)").bitcast(F32), 0.0)
+
+        zero_low_tiles(0)
         bias_of_head = []
         for h in range(H):
             slope = 2.0 ** (-8.0 / H * (h + 1))
@@ -250,43 +253,40 @@ def tile_selfattention_pa_t_kernel(tc, x, Wv, bv, q, k, out):
             )
             v_mx[b] = (v_codes, v_scales)
 
-        def transpose_q(n, halves=(0, 1)):
+        def transpose_rows(rows, slots, words):
+            count = len(slots)
+            t_ps = psum.tile([P, count, P], F32, tag="bank")
+            for u in range(count):
+                nc.tensor.transpose(
+                    out=t_ps[:, u, :], in_=rows[:, slots[u], :].bitcast(F32), identity=ident_f32[:]
+                )
+            nc.scalar.copy(
+                out=words.rearrange("w (p u) -> w p u", u=count), in_=t_ps[:].rearrange("w u p -> w p u")
+            )
+
+        def transpose_q(n, half=None):
             if not live(n):
                 return
             if n not in q_t_of:
                 q_t = work.tile([P, 2 * S], BF16, bufs=3)
                 q_t_of[n] = q_t
-            first, count = 2 * halves[0], 2 * len(halves)
-            qt_ps = psum.tile([P, count, P], F32, tag="bank")
-            for a in range(count):
-                nc.tensor.transpose(
-                    out=qt_ps[:, a, :], in_=q_rows[n][:, first + a, :].bitcast(F32), identity=ident_f32[:]
-                )
-            nc.scalar.copy(
-                out=q_t_of[n][:].bitcast(F32)[:, P * first : P * (first + count)],
-                in_=qt_ps[:].rearrange("w a i -> w (a i)"),
-            )
+            words = q_t_of[n][:].bitcast(F32)
+            if half is None:
+                transpose_rows(q_rows[n], range(Q_TILES), words)
+            else:
+                transpose_rows(q_rows[n], (2 * half, 2 * half + 1), words[:, 2 * P * half : 2 * P * (half + 1)])
 
-        def transpose_k(n, halves=(0, 1)):
+        def transpose_k(n, half=None):
             if not live(n):
                 return
             if n not in k_t_of:
                 k_t = work.tile([P, 2 * S], BF16, bufs=3)
                 k_t_of[n] = k_t
-            count = len(halves)
-            kt_ps = psum.tile([P, count, 2, P], F32, tag="bank")
-            for a in range(count):
-                for u in range(2):
-                    nc.tensor.transpose(
-                        out=kt_ps[:, a, u, :],
-                        in_=k_rows[n][:, halves[a], u, :].bitcast(F32),
-                        identity=ident_f32[:],
-                    )
-            keys = slice(2 * P * halves[0], 2 * P * (halves[0] + count))
-            nc.scalar.copy(
-                out=k_t_of[n][:].bitcast(F32)[:, keys].rearrange("w (half r u) -> w half r u", half=count, u=2),
-                in_=kt_ps[:].rearrange("w half u r -> w half r u"),
-            )
+            words = k_t_of[n][:].bitcast(F32)
+            if half is None:
+                transpose_rows(k_rows[n], range(Q_TILES), words)
+            else:
+                transpose_rows(k_rows[n], (2 * half, 2 * half + 1), words[:, 2 * P * half : 2 * P * (half + 1)])
 
         def score_tile(n, it):
             if not live(n):
@@ -439,7 +439,7 @@ def tile_selfattention_pa_t_kernel(tc, x, Wv, bv, q, k, out):
                     start=True,
                     stop=True,
                 )
-            ctx_sb = work.tile([P, 2, HD], F32, bufs=6)
+            ctx_sb = work.tile([P, 2, HD], F32, bufs=HEADS)
             for a in range(2):
                 it = 2 * pair + a
                 inv = inv_of[b][:, h, it : it + 1]
@@ -450,10 +450,10 @@ def tile_selfattention_pa_t_kernel(tc, x, Wv, bv, q, k, out):
             rows = slice(2 * P * pair, 2 * P * (pair + 1))
             nc.sync.dma_start(out=out[b, rows, dims].rearrange("(a p) d -> p a d", p=P), in_=ctx_sb[:])
 
-        transpose_q(0, (0,))
-        transpose_k(0, (0,))
-        transpose_q(0, (1,))
-        transpose_k(0, (1,))
+        transpose_q(0, 0)
+        transpose_k(0, 0)
+        transpose_q(0, 1)
+        transpose_k(0, 1)
         score_tile(0, 1)
         score_tile(0, 0)
         score_tile(0, 3)
@@ -476,6 +476,8 @@ def tile_selfattention_pa_t_kernel(tc, x, Wv, bv, q, k, out):
         transpose_e(0, 1)
         score_tile(1, 1)
         transpose_e(0, 0)
+        zero_low_tiles(1)
+        zero_low_tiles(2)
         exponential(1, 2)
         transpose_q(2)
         exponential(1, 1)

@@ -11,7 +11,6 @@ U8 = mybir.dt.uint8
 FP8X4 = mybir.dt.float8_e4m3fn_x4
 ALU = mybir.AluOpType
 ACT = mybir.ActivationFunctionType
-AXIS = mybir.AxisListType
 
 B, S, D, H = 8, 512, 512, 2
 HD = D // H
@@ -23,7 +22,6 @@ SCORE_SCALE = 1.0 / math.sqrt(HD)
 MASKED = -3.0e38
 E_COPIES = 3
 PSUM_BANKS = 8
-VECTOR_BIAS_TILES = 1
 
 FLOPS = 2 * B * S * D * D + 2 * (2 * B * H * S * S * HD)
 
@@ -81,11 +79,11 @@ def tile_selfattention_pa_t_kernel(tc, x, Wv, bv, q, k, out):
                 )
                 x_rows.append(x_sb)
             if n == 1:
-                nc.sync.dma_start(out=bv_row[0:1, :], in_=bv.rearrange("(o n) -> o n", o=1))
                 nc.sync.dma_start(
                     out=wv_raw[:].rearrange("w (u e) n -> w u e n", u=2),
                     in_=Wv.rearrange("(u w e) n -> w u e n", u=2, e=2),
                 )
+                nc.sync.dma_start(out=bv_row[0:1, :], in_=bv.rearrange("(o n) -> o n", o=1))
 
         ident_f32 = const.tile([P, P], F32)
         make_identity(nc, ident_f32[:])
@@ -136,14 +134,6 @@ def tile_selfattention_pa_t_kernel(tc, x, Wv, bv, q, k, out):
             bias_bf16 = const.tile([P, S], BF16, name="bias_bf16_%d" % h)
             nc.vector.tensor_scalar_mul(out=bias_bf16[:], in0=bias_f32[:], scalar1=slope / SCORE_SCALE)
             bias_of_head.append(bias_bf16)
-        neg_bias_of_head = []
-        for h in range(H):
-            slope = 2.0 ** (-8.0 / H * (h + 1))
-            neg_bias = const.tile([P, VECTOR_BIAS_TILES * P], F32, name="neg_bias_%d" % h)
-            nc.vector.tensor_scalar_mul(
-                out=neg_bias[:], in0=bias_f32[:, S - VECTOR_BIAS_TILES * P :], scalar1=-slope
-            )
-            neg_bias_of_head.append(neg_bias)
 
         wv_grouped = const.tile([P, D, PACK], BF16, align_bytes=64)
         for c in range(H):
@@ -295,52 +285,34 @@ def tile_selfattention_pa_t_kernel(tc, x, Wv, bv, q, k, out):
             k_view = k_t_of[n][:].rearrange("w (j e) -> w j e", e=2)
             width = P * (it + 1)
             s_ps = psum.tile([P, S], F32, tag="bank")
-            on_vector = it < VECTOR_BIAS_TILES and n % H == 0
             for e in range(2):
                 nc.tensor.matmul(
                     out=s_ps[:, :width],
                     lhsT=q_view[:, it, :, e],
                     rhs=k_view[:, :width, e],
                     start=(e == 0),
-                    stop=(on_vector and e == 1),
+                    stop=False,
                 )
             neg_s = small.tile([P, S], F32)
             neg_max = small.tile([P, 1], F32)
-            if on_vector:
-                nc.vector.scalar_tensor_tensor(
-                    out=neg_s[:, :width],
-                    in0=s_ps[:, :width],
-                    scalar=-SCORE_SCALE,
-                    in1=neg_bias_of_head[n % H][:, VECTOR_BIAS_TILES * P - width :],
-                    op0=ALU.mult,
-                    op1=ALU.add,
-                )
-            else:
-                nc.tensor.matmul(
-                    out=s_ps[:, :width],
-                    lhsT=ident_bf16[:],
-                    rhs=bias_of_head[n % H][:, S - width :],
-                    start=False,
-                    stop=True,
-                )
-                nc.vector.tensor_scalar(
-                    out=neg_s[:, :width],
-                    in0=s_ps[:, :width],
-                    scalar1=-SCORE_SCALE,
-                    scalar2=None,
-                    op0=ALU.mult,
-                    op1=ALU.min,
-                    accum_out=neg_max[:],
-                )
+            nc.tensor.matmul(
+                out=s_ps[:, :width],
+                lhsT=ident_bf16[:],
+                rhs=bias_of_head[n % H][:, S - width :],
+                start=False,
+                stop=True,
+            )
+            nc.vector.tensor_scalar(
+                out=neg_s[:, :width],
+                in0=s_ps[:, :width],
+                scalar1=-SCORE_SCALE,
+                scalar2=None,
+                op0=ALU.mult,
+                op1=ALU.min,
+                accum_out=neg_max[:],
+            )
             s_of[(n, it)] = neg_s
             neg_max_of[(n, it)] = neg_max
-
-        def row_minimum(n, it):
-            if not live(n) or it >= VECTOR_BIAS_TILES or n % H:
-                return
-            nc.vector.tensor_reduce(
-                out=neg_max_of[(n, it)][:], in_=s_of[(n, it)][:, : P * (it + 1)], op=ALU.min, axis=AXIS.X
-            )
 
         def exponential(n, it):
             if not live(n):
@@ -459,7 +431,6 @@ def tile_selfattention_pa_t_kernel(tc, x, Wv, bv, q, k, out):
         score_tile(0, 3)
         exponential(0, 1)
         transpose_q(1)
-        row_minimum(0, 0)
         transpose_k(1)
         score_tile(0, 2)
         exponential(0, 0)
@@ -486,7 +457,6 @@ def tile_selfattention_pa_t_kernel(tc, x, Wv, bv, q, k, out):
         transpose_x(2)
         project_v(0, 0)
         project_v(0, 1)
-        row_minimum(1, 0)
         exponential(1, 0)
         project_v(1, 0)
         transpose_q(3)
@@ -511,7 +481,6 @@ def tile_selfattention_pa_t_kernel(tc, x, Wv, bv, q, k, out):
             score_tile(n, 0)
             project_v(n, 0)
             context(n - 3, 1)
-            row_minimum(n, 0)
             exponential(n, 0)
             quantise_e(n - 2)
             context(n - 3, 0)

@@ -73,10 +73,7 @@ def tile_selfattention_pa_t_kernel(tc, x, Wv, bv, q, k, out):
                 continue
             if n == 1 or h == 0:
                 x_sb = loads.tile([P, PACK, D], BF16, bufs=B)
-                nc.sync.dma_start(
-                    out=x_sb[:].rearrange("p (u e) f -> p u e f", u=2),
-                    in_=x[b].rearrange("(u p e) f -> p u e f", u=2, e=2),
-                )
+                nc.sync.dma_start(out=x_sb[:], in_=x[b].rearrange("(p v) f -> p v f", v=PACK))
                 x_rows.append(x_sb)
             if n == 1:
                 nc.sync.dma_start(
@@ -177,18 +174,17 @@ def tile_selfattention_pa_t_kernel(tc, x, Wv, bv, q, k, out):
             if pair == 0:
                 x_grouped = work.tile([P, PACK * S], BF16, align_bytes=64)
                 x_grouped_of[b] = x_grouped
-            x_words = x_grouped_of[b][:].bitcast(F32).rearrange("w (t c u) -> w t c u", t=PACK, u=2)
+            x_words = x_grouped_of[b][:].bitcast(F32).rearrange("w (h o r k) -> w h o r k", h=2, o=2, k=4)
             xt_ps = psum.tile([P, 2, 2, P], F32, tag="bank")
-            for tl in range(2):
-                t = 2 * pair + tl
+            for v in range(2):
                 for u in range(2):
                     nc.tensor.transpose(
-                        out=xt_ps[:, tl, u, :],
-                        in_=x_rows[b][:, t, :].bitcast(F32)[:, P * u : P * (u + 1)],
+                        out=xt_ps[:, v, u, :],
+                        in_=x_rows[b][:, 2 * v + pair, :].bitcast(F32)[:, P * u : P * (u + 1)],
                         identity=ident_f32[:],
                     )
             nc.vector.tensor_copy(
-                out=x_words[:, 2 * pair : 2 * pair + 2], in_=xt_ps[:].rearrange("w t u c -> w t c u")
+                out=x_words[:, :, pair], in_=xt_ps[:].rearrange("w v u (h r) -> w h r (v u)", h=2)
             )
 
         def quantise_x(m):
@@ -362,15 +358,14 @@ def tile_selfattention_pa_t_kernel(tc, x, Wv, bv, q, k, out):
                 out=e_low[:].rearrange("p a m -> p (a m)").bitcast(F32),
                 in_=et_ps[:].rearrange("p a u i -> p (a u i)"),
             )
-            for a in range(2):
-                nc.gpsimd.tensor_scalar(
-                    out=grouped[:, a, :, 0:2],
-                    in0=e_low[:, a, :].rearrange("p (i o) -> p i o", o=2),
-                    scalar1=1.0,
-                    scalar2=0.0,
-                    op0=ALU.mult,
-                    op1=ALU.add,
-                )
+            nc.gpsimd.tensor_scalar(
+                out=grouped[:, :2, :, 0:2],
+                in0=e_low[:].rearrange("p a (i o) -> p a i o", o=2),
+                scalar1=1.0,
+                scalar2=0.0,
+                op0=ALU.mult,
+                op1=ALU.add,
+            )
 
         def quantise_e(n, first=0, last=Q_TILES):
             if not live(n):
@@ -419,8 +414,11 @@ def tile_selfattention_pa_t_kernel(tc, x, Wv, bv, q, k, out):
                     nc.vector.tensor_scalar_mul(out=ctx_sb[:, a, :], in0=c_ps[:, a, :], scalar1=inv)
                 else:
                     nc.scalar.activation(out=ctx_sb[:, a, :], in_=c_ps[:, a, :], func=ACT.Copy, scale=inv)
-            rows = slice(2 * P * pair, 2 * P * (pair + 1))
-            nc.sync.dma_start(out=out[b, rows, dims].rearrange("(a p) d -> p a d", p=P), in_=ctx_sb[:])
+                if n == HEADS - 1:
+                    nc.sync.dma_start(out=out[b, P * it : P * (it + 1), dims], in_=ctx_sb[:, a, :])
+            if n < HEADS - 1:
+                rows = slice(2 * P * pair, 2 * P * (pair + 1))
+                nc.sync.dma_start(out=out[b, rows, dims].rearrange("(a p) d -> p a d", p=P), in_=ctx_sb[:])
 
         transpose_q(0, 0)
         transpose_k(0, 0)
@@ -474,10 +472,10 @@ def tile_selfattention_pa_t_kernel(tc, x, Wv, bv, q, k, out):
             score_tile(n, 1)
             transpose_e(n - 1, 0)
             exponential(n, 2)
+            transpose_x(n + 2)
             transpose_q(n + 2)
             exponential(n, 1)
             transpose_k(n + 2)
-            transpose_x(n + 2)
             score_tile(n, 0)
             project_v(n, 0)
             context(n - 3, 1)

import math
from contextlib import ExitStack

import concourse.mybir as mybir
from concourse.masks import make_identity

F32 = mybir.dt.float32
BF16 = mybir.dt.bfloat16
U32 = mybir.dt.uint32
U8 = mybir.dt.uint8
FP8X4 = mybir.dt.float8_e4m3fn_x4
ALU = mybir.AluOpType
ACT = mybir.ActivationFunctionType

B, S, D, H = 8, 512, 512, 2
HD = D // H
P = 128
PACK = 4
Q_TILES = S // P
HEADS = B * H
SCORE_SCALE = 1.0 / math.sqrt(HD)
MASKED = -3.0e38
E_COPIES = 3
PSUM_BANKS = 8

FLOPS = 2 * B * S * D * D + 2 * (2 * B * H * S * S * HD)


def tile_selfattention_pa_t_kernel(tc, x, Wv, bv, q, k, out):
    nc = tc.nc
    with ExitStack() as ctx:
        const = ctx.enter_context(tc.tile_pool(name="const", bufs=1))
        loads = ctx.enter_context(tc.tile_pool(name="loads", bufs=HEADS))
        work = ctx.enter_context(tc.tile_pool(name="work", bufs=2))
        small = ctx.enter_context(tc.tile_pool(name="small", bufs=8))
        psum = ctx.enter_context(tc.psum_pool(name="psum", bufs=PSUM_BANKS))
        ctx.enter_context(tc.manual_schedule())

        zero = const.tile([P, 1], F32)
        nc.vector.memset(zero[:], 0.0)
        bv_row = const.tile([P, D], BF16)
        nc.vector.memset(bv_row[:], 0.0)
        ones = const.tile([P, P], BF16)
        nc.vector.memset(ones[:], 1.0)
        idle_rhs = const.tile([P, S], BF16)
        nc.vector.memset(idle_rhs[:], 0.0)

        def keep_warm(count):
            idle_ps = psum.tile([P, S], F32, tag="bank")
            for i in range(count):
                nc.tensor.matmul(out=idle_ps[:], lhsT=ones[:], rhs=idle_rhs[:], start=True, stop=True)

        keep_warm(4)

        wv_raw = const.tile([P, PACK, D], BF16)
        x_rows, q_rows, k_rows = [], [], []
        for n in range(HEADS):
            b, h = n // H, n % H
            halves = 2 if n == 0 else 1
            in_row = Q_TILES // halves
            q_sb = loads.tile([P, Q_TILES, HD], BF16)
            q_rows.append(q_sb)
            k_sb = loads.tile([P, Q_TILES, HD], BF16)
            k_rows.append(k_sb)
            for half in range(halves):
                rows = slice(S // halves * half, S // halves * (half + 1))
                slots = slice(in_row * half, in_row * (half + 1))
                for dst, src in ((q_sb, q), (k_sb, k)):
                    nc.sync.dma_start(
                        out=dst[:, slots], in_=src[b, h, rows].rearrange("(p u) d -> p u d", u=in_row)
                    )
            if n == 0:
                continue
            if n == 1 or h == 0:
                x_sb = loads.tile([P, PACK, D], BF16, bufs=B)
                nc.sync.dma_start(out=x_sb[:], in_=x[b].rearrange("(p v) f -> p v f", v=PACK))
                x_rows.append(x_sb)
            if n == 1:
                nc.sync.dma_start(
                    out=wv_raw[:].rearrange("w (u e) n -> w u e n", u=2),
                    in_=Wv.rearrange("(u w e) n -> w u e n", u=2, e=2),
                )
                nc.sync.dma_start(out=bv_row[0:1, :], in_=bv.rearrange("(o n) -> o n", o=1))

        ident_f32 = const.tile([P, P], F32)
        make_identity(nc, ident_f32[:])
        bias_f32 = const.tile([P, S], F32)
        nc.gpsimd.iota(
            bias_f32[:],
            pattern=[[1, S]],
            base=-(S // 2),
            channel_multiplier=0,
            allow_small_or_imprecise_dtypes=True,
        )
        diagonal = bias_f32[:, S - P :]
        nc.gpsimd.affine_select(
            out=diagonal,
            in_=diagonal,
            pattern=[[-1, P]],
            compare_op=ALU.is_ge,
            fill=MASKED,
            base=0,
            channel_multiplier=1,
        )

        one = const.tile([P, 1], F32)
        nc.scalar.activation(out=one[:], in_=zero[:], func=ACT.Exp)

        e_tiles = []
        for i in range(E_COPIES):
            e_sb = const.tile([P, Q_TILES, S], BF16, name="e_sb_%d" % i)
            nc.vector.memset(e_sb[:, 0, P : 2 * P], 0.0)
            nc.vector.memset(e_sb[:, 2, 3 * P :], 0.0)
            e_tiles.append(e_sb)

        ident_bf16 = const.tile([P, P], BF16)
        nc.vector.tensor_copy(out=ident_bf16[:], in_=ident_f32[:])

        e_grouped_tiles = []
        for i in range(E_COPIES):
            e_grouped = const.tile([P, Q_TILES, P, PACK], BF16, align_bytes=64, name="e_grouped_%d" % i)
            e_grouped_tiles.append(e_grouped)

        def zero_low_tiles(i):
            nc.gpsimd.memset(e_grouped_tiles[i][:, :2].rearrange("p a i t -> p (a i t)").bitcast(F32), 0.0)

        zero_low_tiles(0)
        bias_of_head = []
        for h in range(H):
            slope = 2.0 ** (-8.0 / H * (h + 1))
            bias_bf16 = const.tile([P, S], BF16, name="bias_bf16_%d" % h)
            nc.vector.tensor_scalar_mul(out=bias_bf16[:], in0=bias_f32[:], scalar1=slope / SCORE_SCALE)
            bias_of_head.append(bias_bf16)

        wv_grouped = const.tile([P, D, PACK], BF16, align_bytes=64)
        for c in range(H):
            cols = slice(HD * c, HD * (c + 1))
            nc.gpsimd.tensor_scalar(
                out=wv_grouped[:, cols, :],
                in0=wv_raw[:, :, cols].rearrange("w t n -> w n t"),
                scalar1=1.0,
                scalar2=0.0,
                op0=ALU.mult,
                op1=ALU.add,
            )
        wv_codes = const.tile([P, D], U32, align_bytes=64)
        wv_scales = const.tile([P, D], U8, align_bytes=64)

        def quantise_wv():
            nc.vector.quantize_mx(
                out=wv_codes[:].bitcast(FP8X4),
                scales=wv_scales[:],
                in_=wv_grouped[:].rearrange("w n t -> w (n t)"),
            )

        x_grouped_of, x_mx, v_grouped_of, v_mx = {}, {}, {}, {}
        q_t_of, k_t_of, s_of, neg_max_of, sums = {}, {}, {}, {}, {}
        e_mx, inv_of = {}, {}

        def live(n):
            return 0 <= n < HEADS

        bv_all = const.tile([P, D], BF16)

        def spread_bv():
            bv_ps = psum.tile([P, D], F32, tag="bank")
            nc.tensor.matmul(out=bv_ps[:], lhsT=ones[:], rhs=bv_row[:], start=True, stop=True)
            nc.scalar.copy(out=bv_all[:], in_=bv_ps[:])

        def transpose_x(m):
            if not live(m):
                return
            b, pair = m // 2, m % 2
            if pair == 0:
                x_grouped = work.tile([P, PACK * S], BF16, align_bytes=64)
                x_grouped_of[b] = x_grouped
            x_words = x_grouped_of[b][:].bitcast(F32).rearrange("w (h o r k) -> w h o r k", h=2, o=2, k=4)
            xt_ps = psum.tile([P, 2, 2, P], F32, tag="bank")
            for v in range(2):
                for u in range(2):
                    nc.tensor.transpose(
                        out=xt_ps[:, v, u, :],
                        in_=x_rows[b][:, 2 * v + pair, :].bitcast(F32)[:, P * u : P * (u + 1)],
                        identity=ident_f32[:],
                    )
            nc.vector.tensor_copy(
                out=x_words[:, :, pair], in_=xt_ps[:].rearrange("w v u (h r) -> w h r (v u)", h=2)
            )

        def quantise_x(m):
            if not live(m) or m % 2 == 0:
                return
            b = m // 2
            x_codes = work.tile([P, S], U32, align_bytes=64)
            x_scales = work.tile([P, S], U8, align_bytes=64)
            nc.vector.quantize_mx(
                out=x_codes[:].bitcast(FP8X4), scales=x_scales[:], in_=x_grouped_of[b][:]
            )
            x_mx[b] = (x_codes, x_scales)

        def project_v(m, j):
            if not live(m):
                return
            b, c = m // 2, 2 * (m % 2) + j
            x_codes, x_scales = x_mx[b]
            if c == 0:
                v_grouped = work.tile([P, D, PACK], BF16, align_bytes=64)
                v_grouped_of[b] = v_grouped
            cols = slice(P * c, P * (c + 1))
            v_ps = psum.tile([P, PACK, P], F32, tag="bank")
            for t in range(PACK):
                keys = slice(P * t, P * (t + 1))
                nc.tensor.matmul_mx(
                    out=v_ps[:, t, :],
                    lhsT=x_codes[:, keys].bitcast(FP8X4),
                    lhsT_scale=x_scales[:, keys],
                    rhs=wv_codes[:, cols].bitcast(FP8X4),
                    rhs_scale=wv_scales[:, cols],
                    start=True,
                    stop=True,
                )
            nc.vector.tensor_tensor(
                out=v_grouped_of[b][:, cols, :],
                in0=v_ps[:].rearrange("p t n -> p n t"),
                in1=bv_all[:, cols].unsqueeze(2).to_broadcast([P, P, PACK]),
                op=ALU.add,
            )

        def quantise_v(m):
            if not live(m) or m % 2 == 0:
                return
            b = m // 2
            v_codes = work.tile([P, D], U32, align_bytes=64)
            v_scales = work.tile([P, D], U8, align_bytes=64)
            nc.vector.quantize_mx(
                out=v_codes[:].bitcast(FP8X4),
                scales=v_scales[:],
                in_=v_grouped_of[b][:].rearrange("p n t -> p (n t)"),
            )
            v_mx[b] = (v_codes, v_scales)

        def transpose_rows(rows, slots, words):
            count = len(slots)
            t_ps = psum.tile([P, count, P], F32, tag="bank")
            for u in range(count):
                nc.tensor.transpose(
                    out=t_ps[:, u, :], in_=rows[:, slots[u], :].bitcast(F32), identity=ident_f32[:]
                )
            nc.scalar.copy(
                out=words.rearrange("w (p u) -> w p u", u=count), in_=t_ps[:].rearrange("w u p -> w p u")
            )

        def transpose_q(n, half=None):
            if not live(n):
                return
            if n not in q_t_of:
                q_t = work.tile([P, 2 * S], BF16, bufs=3)
                q_t_of[n] = q_t
            words = q_t_of[n][:].bitcast(F32)
            if half is None:
                transpose_rows(q_rows[n], range(Q_TILES), words)
            else:
                transpose_rows(q_rows[n], (2 * half, 2 * half + 1), words[:, 2 * P * half : 2 * P * (half + 1)])

        def transpose_k(n, half=None):
            if not live(n):
                return
            if n not in k_t_of:
                k_t = work.tile([P, 2 * S], BF16, bufs=3)
                k_t_of[n] = k_t
            words = k_t_of[n][:].bitcast(F32)
            if half is None:
                transpose_rows(k_rows[n], range(Q_TILES), words)
            else:
                transpose_rows(k_rows[n], (2 * half, 2 * half + 1), words[:, 2 * P * half : 2 * P * (half + 1)])

        def score_tile(n, it):
            if not live(n):
                return
            q_view = q_t_of[n][:].rearrange("w (a i e) -> w a i e", a=Q_TILES, e=2)
            k_view = k_t_of[n][:].rearrange("w (j e) -> w j e", e=2)
            width = P * (it + 1)
            s_ps = psum.tile([P, S], F32, tag="bank")
            for e in range(2):
                nc.tensor.matmul(
                    out=s_ps[:, :width],
                    lhsT=q_view[:, it, :, e],
                    rhs=k_view[:, :width, e],
                    start=(e == 0),
                    stop=False,
                )
            neg_s = small.tile([P, S], F32)
            neg_max = small.tile([P, 1], F32)
            nc.tensor.matmul(
                out=s_ps[:, :width],
                lhsT=ident_bf16[:],
                rhs=bias_of_head[n % H][:, S - width :],
                start=False,
                stop=True,
            )
            nc.vector.tensor_scalar(
                out=neg_s[:, :width],
                in0=s_ps[:, :width],
                scalar1=-SCORE_SCALE,
                scalar2=None,
                op0=ALU.mult,
                op1=ALU.min,
                accum_out=neg_max[:],
            )
            s_of[(n, it)] = neg_s
            neg_max_of[(n, it)] = neg_max

        def exponential(n, it):
            if not live(n):
                return
            b, h = n // H, n % H
            if b not in sums:
                row_sum = small.tile([P, H, Q_TILES], F32)
                sums[b] = row_sum
            width = P * (it + 1)
            nc.scalar.activation(
                out=e_tiles[n % E_COPIES][:, it, :width],
                in_=s_of[(n, it)][:, :width],
                func=ACT.Exp,
                bias=neg_max_of[(n, it)][:],
                scale=-1.0,
                accum_out=sums[b][:, h, it : it + 1],
            )

        def transpose_e(n, pair, by_scalar=False):
            if not live(n):
                return
            units = pair + 1
            et_ps = psum.tile([P, 2, units, P], F32, tag="bank")
            for a in range(2):
                for u in range(units):
                    nc.tensor.transpose(
                        out=et_ps[:, a, u, :],
                        in_=e_tiles[n % E_COPIES][:, 2 * pair + a, :].bitcast(F32)[:, P * u : P * (u + 1)],
                        identity=ident_f32[:],
                    )
            grouped = e_grouped_tiles[n % E_COPIES]
            if pair == 1:
                nc.scalar.copy(
                    out=grouped[:, 2:].rearrange("p a i t -> p (a i t)").bitcast(F32).rearrange(
                        "p (a i u) -> p a i u", a=2, u=2
                    ),
                    in_=et_ps[:].rearrange("p a u i -> p a i u"),
                )
                return
            if by_scalar:
                for a in range(2):
                    words = grouped[:, a].rearrange("p i t -> p (i t)").bitcast(F32)
                    nc.scalar.copy(out=words.rearrange("p (i u) -> p i u", u=2)[:, :, 0], in_=et_ps[:, a, 0, :])
                return
            e_low = work.tile([P, 2, 2 * P], BF16)
            nc.scalar.copy(
                out=e_low[:].rearrange("p a m -> p (a m)").bitcast(F32),
                in_=et_ps[:].rearrange("p a u i -> p (a u i)"),
            )
            nc.gpsimd.tensor_scalar(
                out=grouped[:, :2, :, 0:2],
                in0=e_low[:].rearrange("p a (i o) -> p a i o", o=2),
                scalar1=1.0,
                scalar2=0.0,
                op0=ALU.mult,
                op1=ALU.add,
            )

        def quantise_e(n, first=0, last=Q_TILES):
            if not live(n):
                return
            if n not in e_mx:
                e_codes = work.tile([P, S], U32, align_bytes=64)
                e_scales = work.tile([P, S], U8, align_bytes=64)
                e_mx[n] = (e_codes, e_scales)
            e_codes, e_scales = e_mx[n]
            queries = slice(P * first, P * last)
            nc.vector.quantize_mx(
                out=e_codes[:, queries].bitcast(FP8X4),
                scales=e_scales[:, queries],
                in_=e_grouped_tiles[n % E_COPIES][:, first:last].rearrange("p it i t -> p (it i t)"),
            )

        def context(n, pair, by_vector=False):
            if not live(n):
                return
            b, h = n // H, n % H
            e_codes, e_scales = e_mx[n]
            v_codes, v_scales = v_mx[b]
            dims = slice(HD * h, HD * (h + 1))
            if b not in inv_of:
                inv_sum = small.tile([P, H, Q_TILES], F32)
                nc.vector.reciprocal(out=inv_sum[:], in_=sums[b][:])
                inv_of[b] = inv_sum
            c_ps = psum.tile([P, 2, HD], F32, tag="bank")
            for a in range(2):
                it = 2 * pair + a
                queries = slice(P * it, P * (it + 1))
                nc.tensor.matmul_mx(
                    out=c_ps[:, a, :],
                    lhsT=e_codes[:, queries].bitcast(FP8X4),
                    lhsT_scale=e_scales[:, queries],
                    rhs=v_codes[:, dims].bitcast(FP8X4),
                    rhs_scale=v_scales[:, dims],
                    start=True,
                    stop=True,
                )
            ctx_sb = work.tile([P, 2, HD], F32, bufs=HEADS)
            for a in range(2):
                it = 2 * pair + a
                inv = inv_of[b][:, h, it : it + 1]
                if by_vector:
                    nc.vector.tensor_scalar_mul(out=ctx_sb[:, a, :], in0=c_ps[:, a, :], scalar1=inv)
                else:
                    nc.scalar.activation(out=ctx_sb[:, a, :], in_=c_ps[:, a, :], func=ACT.Copy, scale=inv)
                if n == HEADS - 1:
                    nc.sync.dma_start(out=out[b, P * it : P * (it + 1), dims], in_=ctx_sb[:, a, :])
            if n < HEADS - 1:
                rows = slice(2 * P * pair, 2 * P * (pair + 1))
                nc.sync.dma_start(out=out[b, rows, dims].rearrange("(a p) d -> p a d", p=P), in_=ctx_sb[:])

        transpose_q(0, 0)
        transpose_k(0, 0)
        transpose_q(0, 1)
        transpose_k(0, 1)
        score_tile(0, 1)
        score_tile(0, 0)
        score_tile(0, 3)
        exponential(0, 1)
        transpose_q(1)
        transpose_k(1)
        score_tile(0, 2)
        exponential(0, 0)
        transpose_x(0)
        transpose_x(1)
        exponential(0, 3)
        spread_bv()
        score_tile(1, 3)
        score_tile(1, 2)
        exponential(0, 2)
        exponential(1, 3)
        quantise_x(1)
        quantise_wv()
        transpose_e(0, 1)
        score_tile(1, 1)
        transpose_e(0, 0)
        zero_low_tiles(1)
        zero_low_tiles(2)
        exponential(1, 2)
        transpose_q(2)
        exponential(1, 1)
        transpose_k(2)
        score_tile(1, 0)
        transpose_x(2)
        project_v(0, 0)
        project_v(0, 1)
        exponential(1, 0)
        project_v(1, 0)
        transpose_q(3)
        transpose_k(3)
        transpose_x(3)
        project_v(1, 1)

        for n in range(2, HEADS):
            score_tile(n, 3)
            score_tile(n, 2)
            transpose_e(n - 1, 1)
            exponential(n, 3)
            quantise_x(n + 1)
            quantise_v(n - 2)
            score_tile(n, 1)
            transpose_e(n - 1, 0)
            exponential(n, 2)
            transpose_x(n + 2)
            transpose_q(n + 2)
            exponential(n, 1)
            transpose_k(n + 2)
            score_tile(n, 0)
            project_v(n, 0)
            context(n - 3, 1)
            exponential(n, 0)
            quantise_e(n - 2)
            context(n - 3, 0)
            project_v(n, 1)

        last = HEADS - 1
        transpose_e(last, 1)
        quantise_v(last)
        context(last - 2, 1)
        quantise_e(last - 1)
        transpose_e(last, 0, by_scalar=True)
        context(last - 2, 0, by_vector=True)
        context(last - 1, 1)
        quantise_e(last, 2, 4)
        context(last - 1, 0, by_vector=True)
        quantise_e(last, 0, 2)
        context(last, 1)
        context(last, 0, by_vector=True)
